import numpy as np
import ml_dtypes


def mxq(x, axis, fmt="e4m3"):
    dtype, down = {"e4m3": (ml_dtypes.float8_e4m3fn, 7), "e5m2": (ml_dtypes.float8_e5m2, 14)}[fmt]
    v = np.moveaxis(np.asarray(x, np.float32).astype(ml_dtypes.bfloat16).astype(np.float64), axis, -1)
    blocks = v.reshape(v.shape[:-1] + (-1, 32))
    amax = np.abs(blocks).max(-1, keepdims=True)
    byte = np.maximum(np.where(amax > 0, np.frexp(amax)[1] - 1 + 127, 0) - down, 1)
    scale = np.exp2(byte - 127.0)
    codes = (blocks / scale).astype(np.float32).astype(dtype).astype(np.float64)
    return np.moveaxis((codes * scale).reshape(v.shape), -1, axis)


WIDE = False


def mx_kscale(k):
    if not WIDE:
        return np.ones(k)
    levels = np.array([10, -10, 5, -5, 0])
    a = np.random.permutation(np.resize(levels, k // 512 * 4)).reshape(k // 512, 4)
    idx = np.arange(k)
    return np.exp2(a[idx // 512, idx % 128 // 32])


BF16 = ml_dtypes.bfloat16


def bf(x):
    return np.asarray(x, np.float32).astype(BF16)


def f64(x):
    return np.asarray(x).astype(np.float64)


B, S, D, HD, DEPTH = 16, 512, 512, 128, 12
HD2 = 2 * HD
LAMBDA_INIT = 0.8 - 0.6 * np.exp(-0.3 * DEPTH)


def softmax(a):
    e = np.exp(a - a.max(-1, keepdims=True))
    return e / e.sum(-1, keepdims=True)


def setup_inputs():
    s = mx_kscale(D)
    ls = np.sqrt(0.5 / HD)

    def lam_vec(sign):
        return bf(sign * ls * (1.0 + 0.5 * np.random.standard_normal(HD)))

    return {"x": bf(np.random.standard_normal((B, S, D)) * s),
            "q": bf(np.random.standard_normal((B, S, HD2)) * 1.4),
            "k": bf(np.random.standard_normal((B, S, HD2)) * 1.4),
            "WV": bf(np.random.standard_normal((D, HD2)) / np.sqrt(D) / s[:, None]),
            "lambda_q1": lam_vec(1.0), "lambda_q2": lam_vec(1.0),
            "lambda_k1": lam_vec(1.0), "lambda_k2": lam_vec(-1.0)}


def reference(x, q, k, WV, lambda_q1, lambda_q2, lambda_k1, lambda_k2):
    scale = HD ** -0.5
    v = mxq(f64(x), 2, "e4m3") @ mxq(f64(WV), 0, "e4m3")
    a1 = f64(q)[..., :HD] @ f64(k)[..., :HD].transpose(0, 2, 1) * scale
    a2 = f64(q)[..., HD:] @ f64(k)[..., HD:].transpose(0, 2, 1) * scale
    lambda_1 = np.exp(np.sum(f64(lambda_q1) * f64(lambda_k1)))
    lambda_2 = np.exp(np.sum(f64(lambda_q2) * f64(lambda_k2)))
    lam = lambda_1 + lambda_2 + LAMBDA_INIT
    attn = softmax(a1) - lam * softmax(a2)
    return mxq(attn, 2, "e4m3") @ mxq(v, 1, "e4m3")

@@ -1,0 +1,288 @@
+import math
+from contextlib import ExitStack
+
+import concourse.mybir as mybir
+from concourse.masks import make_identity
+
+F32 = mybir.dt.float32
+BF16 = mybir.dt.bfloat16
+U32 = mybir.dt.uint32
+U8 = mybir.dt.uint8
+FP8X4 = mybir.dt.float8_e4m3fn_x4
+ALU = mybir.AluOpType
+ACT = mybir.ActivationFunctionType
+AXIS_X = mybir.AxisListType.X
+
+P = 128
+B, S, D, HD = 16, 512, 512, 128
+HD2 = 2 * HD
+TILES = S // P
+SCALE = HD**-0.5
+LAMBDA_INIT = 0.8 - 0.6 * math.exp(-0.3 * 12)
+
+FLOPS = B * (2 * S * D * HD2 + 2 * 2 * S * S * HD + 2 * S * S * HD2)
+
+
+def tile_differentialattention_pa_t_kernel(
+    tc, x, q, k, WV, lambda_q1, lambda_q2, lambda_k1, lambda_k2, out
+):
+    nc = tc.nc
+    with ExitStack() as stack:
+        const = stack.enter_context(tc.tile_pool(name="const", bufs=1))
+        loads = stack.enter_context(tc.tile_pool(name="loads", bufs=3))
+        batch = stack.enter_context(tc.tile_pool(name="batch", bufs=2))
+        work = stack.enter_context(tc.tile_pool(name="work", bufs=3))
+        small = stack.enter_context(tc.tile_pool(name="small", bufs=4))
+        psum = stack.enter_context(tc.psum_pool(name="psum", bufs=2))
+
+        ident_bf16 = const.tile([P, P], BF16)
+        make_identity(nc, ident_bf16[:])
+        ident_f32 = const.tile([P, P], F32)
+        make_identity(nc, ident_f32[:])
+
+        wv_rows = const.tile([P, 4, HD2], BF16)
+        nc.scalar.dma_start(
+            out=wv_rows[:].rearrange("p (g e) c -> p g (e c)", g=2),
+            in_=WV.rearrange("(g p e) c -> p g (e c)", g=2, e=2),
+        )
+        wv_grouped = const.tile([P, HD2, 4], BF16, align_bytes=64)
+        nc.vector.tensor_copy(out=wv_grouped[:], in_=wv_rows[:].rearrange("p t c -> p c t"))
+        wv_codes = const.tile([P, HD2], U32, align_bytes=64)
+        wv_scales = const.tile([P, HD2], U8, align_bytes=64)
+        nc.vector.quantize_mx(
+            out=wv_codes[:].bitcast(FP8X4),
+            scales=wv_scales[:],
+            in_=wv_grouped[:].rearrange("p c t -> p (c t)"),
+        )
+
+        lam_vecs = const.tile([P, 4, HD], BF16)
+        for i, vec in enumerate((lambda_q1, lambda_q2, lambda_k1, lambda_k2)):
+            nc.scalar.dma_start(out=lam_vecs[:, i, :], in_=vec.partition_broadcast(P))
+        lam_prod = const.tile([P, 2, HD], F32)
+        nc.vector.tensor_tensor(
+            out=lam_prod[:], in0=lam_vecs[:, 0:2, :], in1=lam_vecs[:, 2:4, :], op=ALU.mult
+        )
+        lam_dots = const.tile([P, 2], F32)
+        nc.vector.reduce_sum(out=lam_dots[:], in_=lam_prod[:], axis=AXIS_X)
+        lam_exps = const.tile([P, 2], F32)
+        lam_sum = const.tile([P, 1], F32)
+        nc.scalar.activation(out=lam_exps[:], in_=lam_dots[:], func=ACT.Exp, accum_out=lam_sum[:])
+        neg_lam = const.tile([P, 1], F32)
+        nc.vector.tensor_scalar(
+            out=neg_lam[:], in0=lam_sum[:], scalar1=LAMBDA_INIT, scalar2=-1.0,
+            op0=ALU.add, op1=ALU.mult,
+        )
+
+        loaded = {}
+        heads = {}
+        x_mx = {}
+        v_mx = {}
+        a_mx = {}
+        scores = {}
+        shifts = {}
+        exps = {}
+        attn_T = {}
+
+        def load(b):
+            k_sb = loads.tile([P, TILES, HD2], BF16)
+            nc.sync.dma_start(out=k_sb[:], in_=k[b].rearrange("(m i) d -> i m d", i=P))
+            q_sb = loads.tile([P, TILES, HD2], BF16)
+            nc.sync.dma_start(out=q_sb[:], in_=q[b].rearrange("(p j) d -> p j d", j=TILES))
+            x_sb = loads.tile([P, TILES * D], BF16)
+            nc.sync.dma_start(
+                out=x_sb[:].rearrange("r (u f) -> r u f", u=2),
+                in_=x[b].rearrange("(u r e) d -> r u (e d)", u=2, e=2),
+            )
+            loaded[b] = (x_sb, q_sb, k_sb)
+
+        def transpose_qk(b):
+            x_sb, q_sb, k_sb = loaded[b]
+            transposed = []
+            for name, rows in (("qT", q_sb), ("kT", k_sb)):
+                t_ps = psum.tile([P, 2, TILES, P], BF16, name=name + "_ps", tag="aux", bufs=2)
+                for h in range(2):
+                    for j in range(TILES):
+                        nc.tensor.transpose(
+                            t_ps[:, h, j, :], rows[:, j, h * HD : (h + 1) * HD], ident_bf16[:]
+                        )
+                t_sb = batch.tile([P, 2, TILES, P], BF16, name=name, tag=name)
+                nc.scalar.copy(out=t_sb[:], in_=t_ps[:])
+                transposed.append(t_sb)
+            heads[b] = transposed
+
+        def transpose_x(b):
+            x_sb, q_sb, k_sb = loaded.pop(b)
+            x_words = x_sb[:].bitcast(F32)
+            x_grouped = batch.tile([P, TILES * P * 4], BF16, align_bytes=64)
+            x_grouped_words = x_grouped[:].bitcast(F32).rearrange(
+                "p (t r g) -> p t r g", t=TILES, g=2
+            )
+            for pair in range(TILES // 2):
+                xT_ps = psum.tile([P, 2, 2, P], F32, tag="aux", bufs=2)
+                for i in range(2):
+                    t = 2 * pair + i
+                    for g in range(2):
+                        first = t * (D // 2) + g * P
+                        nc.tensor.transpose(
+                            xT_ps[:, i, g, :], x_words[:, first : first + P], ident_f32[:]
+                        )
+                nc.scalar.copy(
+                    out=x_grouped_words[:, 2 * pair : 2 * pair + 2, :, :],
+                    in_=xT_ps[:].rearrange("p t g r -> p t r g"),
+                )
+            x_mx[b] = x_grouped
+
+        def quantise(grouped, width, name):
+            codes = batch.tile([P, width], U32, name=name + "_codes", align_bytes=64)
+            scales = batch.tile([P, width], U8, name=name + "_scales", align_bytes=64)
+            nc.vector.quantize_mx(out=codes[:].bitcast(FP8X4), scales=scales[:], in_=grouped)
+            return codes, scales
+
+        def project_v(b):
+            x_codes, x_scales = x_mx.pop(b)
+            v_grouped = batch.tile([P, HD2, TILES], BF16, align_bytes=64)
+            for half in range(2):
+                cols = slice(half * P, (half + 1) * P)
+                v_ps = psum.tile([P, TILES, P], F32, tag="aux", bufs=2)
+                for t in range(TILES):
+                    toks = slice(t * P, (t + 1) * P)
+                    nc.tensor.matmul_mx(
+                        out=v_ps[:, t, :],
+                        lhsT=x_codes[:, toks].bitcast(FP8X4),
+                        lhsT_scale=x_scales[:, toks],
+                        rhs=wv_codes[:, cols].bitcast(FP8X4),
+                        rhs_scale=wv_scales[:, cols],
+                        start=True,
+                        stop=True,
+                    )
+                nc.scalar.copy(out=v_grouped[:, cols, :], in_=v_ps[:].rearrange("p t c -> p c t"))
+            v_mx[b] = v_grouped
+
+        def output(b):
+            a_codes, a_scales = a_mx.pop(b)
+            v_codes, v_scales = v_mx.pop(b)
+            out_sb = batch.tile([P, TILES, HD2], F32)
+            for pair in range(TILES // 2):
+                o_ps = psum.tile([P, 2, HD2], F32, tag="aux", bufs=2)
+                for i in range(2):
+                    rows = slice((2 * pair + i) * P, (2 * pair + i + 1) * P)
+                    nc.tensor.matmul_mx(
+                        out=o_ps[:, i, :],
+                        lhsT=a_codes[:, rows].bitcast(FP8X4),
+                        lhsT_scale=a_scales[:, rows],
+                        rhs=v_codes[:].bitcast(FP8X4),
+                        rhs_scale=v_scales[:],
+                        start=True,
+                        stop=True,
+                    )
+                nc.scalar.copy(out=out_sb[:, 2 * pair : 2 * pair + 2, :], in_=o_ps[:])
+            nc.sync.dma_start(out=out[b].rearrange("(p j) c -> p j c", j=TILES), in_=out_sb[:])
+
+        def score_matmuls(step):
+            b, j = divmod(step, TILES)
+            qT, kT = heads[b]
+            banks = []
+            for h in range(2):
+                s_ps = psum.tile([P, S], F32, name="s_ps", tag="scores", bufs=4)
+                nc.tensor.matmul(
+                    out=s_ps[:],
+                    lhsT=qT[:, h, j, :],
+                    rhs=kT[:, h, :, :].rearrange("p m i -> p (m i)"),
+                    start=True,
+                    stop=True,
+                )
+                banks.append(s_ps)
+            scores[step] = banks
+
+        def row_maxima(step):
+            row_max = small.tile([P, 2], F32)
+            for h in range(2):
+                nc.vector.reduce_max(out=row_max[:, h : h + 1], in_=scores[step][h][:], axis=AXIS_X)
+            shift = small.tile([P, 2], F32)
+            nc.vector.tensor_scalar_mul(out=shift[:], in0=row_max[:], scalar1=-SCALE)
+            shifts[step] = shift
+
+        def exponentials(step):
+            banks = scores.pop(step)
+            shift = shifts.pop(step)
+            expd = work.tile([P, 2, S], F32)
+            row_sum = small.tile([P, 2], F32)
+            for h in range(2):
+                nc.scalar.activation(
+                    out=expd[:, h, :],
+                    in_=banks[h][:],
+                    func=ACT.Exp,
+                    bias=shift[:, h : h + 1],
+                    scale=SCALE,
+                    accum_out=row_sum[:, h : h + 1],
+                )
+            exps[step] = (expd, row_sum)
+
+        def combine_and_transpose(step):
+            expd, row_sum = exps.pop(step)
+            inv_sum = small.tile([P, 2], F32)
+            nc.vector.reciprocal(out=inv_sum[:], in_=row_sum[:])
+            second = work.tile([P, S], F32)
+            nc.vector.tensor_scalar(
+                out=second[:], in0=expd[:, 1, :], scalar1=inv_sum[:, 1:2], scalar2=neg_lam[:, 0:1],
+                op0=ALU.mult, op1=ALU.mult,
+            )
+            attn = work.tile([P, S], BF16)
+            nc.vector.scalar_tensor_tensor(
+                out=attn[:], in0=expd[:, 0, :], scalar=inv_sum[:, 0:1], in1=second[:],
+                op0=ALU.mult, op1=ALU.add,
+            )
+            attn_words = attn[:].bitcast(F32)
+            aT_ps = psum.tile([P, 2, P], F32, bufs=2)
+            for u in range(2):
+                nc.tensor.transpose(aT_ps[:, u, :], attn_words[:, u * P : (u + 1) * P], ident_f32[:])
+            attn_T[step] = aT_ps
+
+        def copy_attn(step):
+            b, j = divmod(step, TILES)
+            if j == 0:
+                a_mx[b] = batch.tile([P, TILES * P * 4], BF16, name="a_grouped", align_bytes=64)
+            a_grouped_words = a_mx[b][:].bitcast(F32).rearrange("p (j q u) -> p j q u", j=TILES, u=2)
+            aT_ps = attn_T.pop(step)
+            nc.scalar.copy(out=a_grouped_words[:, j, :, :], in_=aT_ps[:].rearrange("p u q -> p q u"))
+
+        STEPS = B * TILES
+
+        def is_step(step):
+            return 0 <= step < STEPS
+
+        def is_batch(b):
+            return 0 <= b < B
+
+        with tc.manual_schedule():
+            load(0)
+            for i in range(-TILES, STEPS + 3):
+                b, quarter = divmod(i, TILES)
+                if is_step(i + 2):
+                    score_matmuls(i + 2)
+                if is_step(i + 1):
+                    row_maxima(i + 1)
+                    exponentials(i + 1)
+                if quarter == 0:
+                    if is_batch(b + 2):
+                        load(b + 2)
+                    if is_batch(b + 1):
+                        transpose_qk(b + 1)
+                    if is_batch(b):
+                        v_mx[b] = quantise(v_mx[b][:].rearrange("p c t -> p (c t)"), HD2, "v")
+                if quarter == 1:
+                    if is_batch(b + 1):
+                        transpose_x(b + 1)
+                    if is_batch(b - 1):
+                        a_mx[b - 1] = quantise(a_mx[b - 1][:], S, "a")
+                if quarter == 2:
+                    if is_batch(b - 1):
+                        output(b - 1)
+                    if is_batch(b + 1):
+                        x_mx[b + 1] = quantise(x_mx[b + 1][:], S, "x")
+                if quarter == 3 and is_batch(b + 1):
+                    project_v(b + 1)
+                if is_step(i):
+                    combine_and_transpose(i)
+                if is_step(i - 1):
+                    copy_attn(i - 1)

@@ -79,8 +79,9 @@ def tile_differentialattention_pa_t_kernel(
         v_mx = {}
         a_mx = {}
         scores = {}
-        shifts = {}
+        maxima = {}
         exps = {}
+        seconds = {}
         attn_T = {}
 
         def load(b):
@@ -198,13 +199,12 @@ def tile_differentialattention_pa_t_kernel(
             row_max = small.tile([P, 2], F32)
             for h in range(2):
                 nc.vector.reduce_max(out=row_max[:, h : h + 1], in_=scores[step][h][:], axis=AXIS_X)
-            shift = small.tile([P, 2], F32)
-            nc.vector.tensor_scalar_mul(out=shift[:], in0=row_max[:], scalar1=-SCALE)
-            shifts[step] = shift
+            maxima[step] = row_max
 
         def exponentials(step):
             banks = scores.pop(step)
-            shift = shifts.pop(step)
+            shift = small.tile([P, 2], F32)
+            nc.vector.tensor_scalar_mul(out=shift[:], in0=maxima.pop(step)[:], scalar1=-SCALE)
             expd = work.tile([P, 2, S], F32)
             row_sum = small.tile([P, 2], F32)
             for h in range(2):
@@ -218,15 +218,24 @@ def tile_differentialattention_pa_t_kernel(
                 )
             exps[step] = (expd, row_sum)
 
-        def combine_and_transpose(step):
-            expd, row_sum = exps.pop(step)
+        def reciprocals(step):
+            expd, row_sum = exps[step]
             inv_sum = small.tile([P, 2], F32)
             nc.vector.reciprocal(out=inv_sum[:], in_=row_sum[:])
+            exps[step] = (expd, inv_sum)
+
+        def scale_second(step):
+            expd, inv_sum = exps[step]
             second = work.tile([P, S], F32)
             nc.vector.tensor_scalar(
                 out=second[:], in0=expd[:, 1, :], scalar1=inv_sum[:, 1:2], scalar2=neg_lam[:, 0:1],
                 op0=ALU.mult, op1=ALU.mult,
             )
+            seconds[step] = second
+
+        def difference_and_transpose(step):
+            expd, inv_sum = exps.pop(step)
+            second = seconds.pop(step)
             attn = work.tile([P, S], BF16)
             nc.vector.scalar_tensor_tensor(
                 out=attn[:], in0=expd[:, 0, :], scalar=inv_sum[:, 0:1], in1=second[:],
@@ -256,33 +265,38 @@ def tile_differentialattention_pa_t_kernel(
 
         with tc.manual_schedule():
             load(0)
-            for i in range(-TILES, STEPS + 3):
+            for i in range(-TILES, STEPS + TILES):
                 b, quarter = divmod(i, TILES)
                 if is_step(i + 2):
                     score_matmuls(i + 2)
                 if is_step(i + 1):
                     row_maxima(i + 1)
+                if is_step(i):
+                    reciprocals(i)
+                if is_step(i + 1):
                     exponentials(i + 1)
+                if is_step(i):
+                    scale_second(i)
                 if quarter == 0:
                     if is_batch(b + 2):
                         load(b + 2)
                     if is_batch(b + 1):
                         transpose_qk(b + 1)
+                    if is_batch(b - 1):
+                        v_mx[b - 1] = quantise(v_mx[b - 1][:].rearrange("p c t -> p (c t)"), HD2, "v")
+                if quarter == 1 and is_batch(b + 1):
+                    transpose_x(b + 1)
+                if quarter == 2:
                     if is_batch(b):
-                        v_mx[b] = quantise(v_mx[b][:].rearrange("p c t -> p (c t)"), HD2, "v")
-                if quarter == 1:
-                    if is_batch(b + 1):
-                        transpose_x(b + 1)
+                        project_v(b)
                     if is_batch(b - 1):
                         a_mx[b - 1] = quantise(a_mx[b - 1][:], S, "a")
-                if quarter == 2:
+                if quarter == 3:
                     if is_batch(b - 1):
                         output(b - 1)
                     if is_batch(b + 1):
                         x_mx[b + 1] = quantise(x_mx[b + 1][:], S, "x")
-                if quarter == 3 and is_batch(b + 1):
-                    project_v(b + 1)
                 if is_step(i):
-                    combine_and_transpose(i)
+                    difference_and_transpose(i)
                 if is_step(i - 1):
                     copy_attn(i - 1)

@@ -227,7 +227,7 @@ def tile_differentialattention_pa_t_kernel(
         def scale_second(step):
             expd, inv_sum = exps[step]
             second = work.tile([P, S], F32)
-            nc.vector.tensor_scalar(
+            nc.gpsimd.tensor_scalar(
                 out=second[:], in0=expd[:, 1, :], scalar1=inv_sum[:, 1:2], scalar2=neg_lam[:, 0:1],
                 op0=ALU.mult, op1=ALU.mult,
             )
@@ -253,7 +253,9 @@ def tile_differentialattention_pa_t_kernel(
                 a_mx[b] = batch.tile([P, TILES * P * 4], BF16, name="a_grouped", align_bytes=64)
             a_grouped_words = a_mx[b][:].bitcast(F32).rearrange("p (j q u) -> p j q u", j=TILES, u=2)
             aT_ps = attn_T.pop(step)
-            nc.scalar.copy(out=a_grouped_words[:, j, :, :], in_=aT_ps[:].rearrange("p u q -> p q u"))
+            nc.vector.tensor_copy(
+                out=a_grouped_words[:, j, :, :], in_=aT_ps[:].rearrange("p u q -> p q u")
+            )
 
         STEPS = B * TILES
 
@@ -269,14 +271,15 @@ def tile_differentialattention_pa_t_kernel(
                 b, quarter = divmod(i, TILES)
                 if is_step(i + 2):
                     score_matmuls(i + 2)
+                if is_step(i - 1):
+                    reciprocals(i - 1)
+                    scale_second(i - 1)
                 if is_step(i + 1):
                     row_maxima(i + 1)
-                if is_step(i):
-                    reciprocals(i)
+                if is_step(i - 2):
+                    copy_attn(i - 2)
                 if is_step(i + 1):
                     exponentials(i + 1)
-                if is_step(i):
-                    scale_second(i)
                 if quarter == 0:
                     if is_batch(b + 2):
                         load(b + 2)
@@ -296,7 +299,5 @@ def tile_differentialattention_pa_t_kernel(
                         output(b - 1)
                     if is_batch(b + 1):
                         x_mx[b + 1] = quantise(x_mx[b + 1][:], S, "x")
-                if is_step(i):
-                    difference_and_transpose(i)
                 if is_step(i - 1):
-                    copy_attn(i - 1)
+                    difference_and_transpose(i - 1)

@@ -78,6 +78,7 @@ def tile_differentialattention_pa_t_kernel(
         x_mx = {}
         v_mx = {}
         a_mx = {}
+        a_pairs = {}
         scores = {}
         maxima = {}
         exps = {}
@@ -99,7 +100,7 @@ def tile_differentialattention_pa_t_kernel(
         def transpose_qk(b):
             x_sb, q_sb, k_sb = loaded[b]
             transposed = []
-            for name, rows in (("qT", q_sb), ("kT", k_sb)):
+            for name, rows in (("kT", k_sb), ("qT", q_sb)):
                 t_ps = psum.tile([P, 2, TILES, P], BF16, name=name + "_ps", tag="aux", bufs=2)
                 for h in range(2):
                     for j in range(TILES):
@@ -109,7 +110,8 @@ def tile_differentialattention_pa_t_kernel(
                 t_sb = batch.tile([P, 2, TILES, P], BF16, name=name, tag=name)
                 nc.scalar.copy(out=t_sb[:], in_=t_ps[:])
                 transposed.append(t_sb)
-            heads[b] = transposed
+            kT, qT = transposed
+            heads[b] = (qT, kT)
 
         def transpose_x(b):
             x_sb, q_sb, k_sb = loaded.pop(b)
@@ -139,45 +141,46 @@ def tile_differentialattention_pa_t_kernel(
             nc.vector.quantize_mx(out=codes[:].bitcast(FP8X4), scales=scales[:], in_=grouped)
             return codes, scales
 
-        def project_v(b):
-            x_codes, x_scales = x_mx.pop(b)
-            v_grouped = batch.tile([P, HD2, TILES], BF16, align_bytes=64)
-            for half in range(2):
-                cols = slice(half * P, (half + 1) * P)
-                v_ps = psum.tile([P, TILES, P], F32, tag="aux", bufs=2)
-                for t in range(TILES):
-                    toks = slice(t * P, (t + 1) * P)
-                    nc.tensor.matmul_mx(
-                        out=v_ps[:, t, :],
-                        lhsT=x_codes[:, toks].bitcast(FP8X4),
-                        lhsT_scale=x_scales[:, toks],
-                        rhs=wv_codes[:, cols].bitcast(FP8X4),
-                        rhs_scale=wv_scales[:, cols],
-                        start=True,
-                        stop=True,
-                    )
-                nc.scalar.copy(out=v_grouped[:, cols, :], in_=v_ps[:].rearrange("p t c -> p c t"))
-            v_mx[b] = v_grouped
+        def project_v(b, half):
+            x_codes, x_scales = x_mx[b]
+            if half == 0:
+                v_mx[b] = batch.tile([P, HD2, TILES], BF16, name="v_grouped", align_bytes=64)
+            cols = slice(half * P, (half + 1) * P)
+            v_ps = psum.tile([P, TILES, P], F32, tag="aux", bufs=2)
+            for t in range(TILES):
+                toks = slice(t * P, (t + 1) * P)
+                nc.tensor.matmul_mx(
+                    out=v_ps[:, t, :],
+                    lhsT=x_codes[:, toks].bitcast(FP8X4),
+                    lhsT_scale=x_scales[:, toks],
+                    rhs=wv_codes[:, cols].bitcast(FP8X4),
+                    rhs_scale=wv_scales[:, cols],
+                    start=True,
+                    stop=True,
+                )
+            nc.scalar.copy(out=v_mx[b][:, cols, :], in_=v_ps[:].rearrange("p t c -> p c t"))
 
-        def output(b):
-            a_codes, a_scales = a_mx.pop(b)
-            v_codes, v_scales = v_mx.pop(b)
-            out_sb = batch.tile([P, TILES, HD2], F32)
-            for pair in range(TILES // 2):
-                o_ps = psum.tile([P, 2, HD2], F32, tag="aux", bufs=2)
-                for i in range(2):
-                    rows = slice((2 * pair + i) * P, (2 * pair + i + 1) * P)
-                    nc.tensor.matmul_mx(
-                        out=o_ps[:, i, :],
-                        lhsT=a_codes[:, rows].bitcast(FP8X4),
-                        lhsT_scale=a_scales[:, rows],
-                        rhs=v_codes[:].bitcast(FP8X4),
-                        rhs_scale=v_scales[:],
-                        start=True,
-                        stop=True,
-                    )
-                nc.scalar.copy(out=out_sb[:, 2 * pair : 2 * pair + 2, :], in_=o_ps[:])
-            nc.sync.dma_start(out=out[b].rearrange("(p j) c -> p j c", j=TILES), in_=out_sb[:])
+        def output(b, pair):
+            a_codes, a_scales = a_pairs.pop((b, pair))
+            v_codes, v_scales = v_mx[b]
+            o_ps = psum.tile([P, 2, HD2], F32, tag="aux", bufs=2)
+            for i in range(2):
+                rows = slice(i * P, (i + 1) * P)
+                nc.tensor.matmul_mx(
+                    out=o_ps[:, i, :],
+                    lhsT=a_codes[:, rows].bitcast(FP8X4),
+                    lhsT_scale=a_scales[:, rows],
+                    rhs=v_codes[:].bitcast(FP8X4),
+                    rhs_scale=v_scales[:],
+                    start=True,
+                    stop=True,
+                )
+            out_sb = batch.tile([P, 2, HD2], F32)
+            nc.scalar.copy(out=out_sb[:], in_=o_ps[:])
+            nc.sync.dma_start(
+                out=out[b].rearrange("(p j) c -> p j c", j=TILES)[:, 2 * pair : 2 * pair + 2, :],
+                in_=out_sb[:],
+            )
 
         def score_matmuls(step):
             b, j = divmod(step, TILES)
@@ -253,9 +256,8 @@ def tile_differentialattention_pa_t_kernel(
                 a_mx[b] = batch.tile([P, TILES * P * 4], BF16, name="a_grouped", align_bytes=64)
             a_grouped_words = a_mx[b][:].bitcast(F32).rearrange("p (j q u) -> p j q u", j=TILES, u=2)
             aT_ps = attn_T.pop(step)
-            nc.vector.tensor_copy(
-                out=a_grouped_words[:, j, :, :], in_=aT_ps[:].rearrange("p u q -> p q u")
-            )
+            copy = nc.scalar.copy if j == 0 else nc.vector.tensor_copy
+            copy(out=a_grouped_words[:, j, :, :], in_=aT_ps[:].rearrange("p u q -> p q u"))
 
         STEPS = B * TILES
 
@@ -286,17 +288,23 @@ def tile_differentialattention_pa_t_kernel(
                     if is_batch(b + 1):
                         transpose_qk(b + 1)
                     if is_batch(b - 1):
+                        a_pairs[(b - 1, 0)] = quantise(a_mx[b - 1][:, 0 : 2 * P * 4], 2 * P, "a")
+                if quarter == 1:
+                    if is_batch(b + 1):
+                        transpose_x(b + 1)
+                    if is_batch(b - 1):
                         v_mx[b - 1] = quantise(v_mx[b - 1][:].rearrange("p c t -> p (c t)"), HD2, "v")
-                if quarter == 1 and is_batch(b + 1):
-                    transpose_x(b + 1)
                 if quarter == 2:
                     if is_batch(b):
-                        project_v(b)
+                        project_v(b, 0)
                     if is_batch(b - 1):
-                        a_mx[b - 1] = quantise(a_mx[b - 1][:], S, "a")
+                        output(b - 1, 0)
+                        a_pairs[(b - 1, 1)] = quantise(a_mx[b - 1][:, 2 * P * 4 :], 2 * P, "a")
                 if quarter == 3:
+                    if is_batch(b):
+                        project_v(b, 1)
                     if is_batch(b - 1):
-                        output(b - 1)
+                        output(b - 1, 1)
                     if is_batch(b + 1):
                         x_mx[b + 1] = quantise(x_mx[b + 1][:], S, "x")
                 if is_step(i - 1):

@@ -82,19 +82,16 @@ def tile_differentialattention_pa_t_kernel(
         scores = {}
         maxima = {}
         exps = {}
-        seconds = {}
+        softmaxes = {}
         attn_T = {}
 
         def load(b):
             k_sb = loads.tile([P, TILES, HD2], BF16)
-            nc.sync.dma_start(out=k_sb[:], in_=k[b].rearrange("(m i) d -> i m d", i=P))
+            nc.sync.dma_start(out=k_sb[:], in_=k[b].rearrange("(p t) d -> p t d", t=TILES))
             q_sb = loads.tile([P, TILES, HD2], BF16)
             nc.sync.dma_start(out=q_sb[:], in_=q[b].rearrange("(p j) d -> p j d", j=TILES))
             x_sb = loads.tile([P, TILES * D], BF16)
-            nc.sync.dma_start(
-                out=x_sb[:].rearrange("r (u f) -> r u f", u=2),
-                in_=x[b].rearrange("(u r e) d -> r u (e d)", u=2, e=2),
-            )
+            nc.sync.dma_start(out=x_sb[:], in_=x[b].rearrange("(p t) d -> p (t d)", t=TILES))
             loaded[b] = (x_sb, q_sb, k_sb)
 
         def transpose_qk(b):
@@ -227,37 +224,41 @@ def tile_differentialattention_pa_t_kernel(
             nc.vector.reciprocal(out=inv_sum[:], in_=row_sum[:])
             exps[step] = (expd, inv_sum)
 
-        def scale_second(step):
-            expd, inv_sum = exps[step]
-            second = work.tile([P, S], F32)
+        def normalise(step):
+            expd, inv_sum = exps.pop(step)
+            normed = work.tile([P, 2, S], F32)
             nc.gpsimd.tensor_scalar(
-                out=second[:], in0=expd[:, 1, :], scalar1=inv_sum[:, 1:2], scalar2=neg_lam[:, 0:1],
+                out=normed[:, 0, :], in0=expd[:, 0, :], scalar1=inv_sum[:, 0:1], scalar2=1.0,
                 op0=ALU.mult, op1=ALU.mult,
             )
-            seconds[step] = second
-
-        def difference_and_transpose(step):
-            expd, inv_sum = exps.pop(step)
-            second = seconds.pop(step)
-            attn = work.tile([P, S], BF16)
-            nc.vector.scalar_tensor_tensor(
-                out=attn[:], in0=expd[:, 0, :], scalar=inv_sum[:, 0:1], in1=second[:],
-                op0=ALU.mult, op1=ALU.add,
+            nc.gpsimd.tensor_scalar(
+                out=normed[:, 1, :], in0=expd[:, 1, :], scalar1=inv_sum[:, 1:2],
+                scalar2=neg_lam[:, 0:1], op0=ALU.mult, op1=ALU.mult,
             )
-            attn_words = attn[:].bitcast(F32)
-            aT_ps = psum.tile([P, 2, P], F32, bufs=2)
-            for u in range(2):
-                nc.tensor.transpose(aT_ps[:, u, :], attn_words[:, u * P : (u + 1) * P], ident_f32[:])
+            softmaxes[step] = normed
+
+        def difference_transposed(step):
+            normed = softmaxes.pop(step)
+            aT_ps = psum.tile([P, TILES, P], F32, bufs=2)
+            for t in range(TILES):
+                for h in range(2):
+                    nc.tensor.matmul(
+                        out=aT_ps[:, t, :],
+                        lhsT=normed[:, h, t * P : (t + 1) * P],
+                        rhs=ident_f32[:],
+                        start=(h == 0),
+                        stop=(h == 1),
+                        is_transpose=True,
+                    )
             attn_T[step] = aT_ps
 
         def copy_attn(step):
             b, j = divmod(step, TILES)
             if j == 0:
                 a_mx[b] = batch.tile([P, TILES * P * 4], BF16, name="a_grouped", align_bytes=64)
-            a_grouped_words = a_mx[b][:].bitcast(F32).rearrange("p (j q u) -> p j q u", j=TILES, u=2)
+            a_grouped = a_mx[b][:].rearrange("p (j q t) -> p j q t", j=TILES, t=TILES)
             aT_ps = attn_T.pop(step)
-            copy = nc.scalar.copy if j == 0 else nc.vector.tensor_copy
-            copy(out=a_grouped_words[:, j, :, :], in_=aT_ps[:].rearrange("p u q -> p q u"))
+            nc.vector.tensor_copy(out=a_grouped[:, j, :, :], in_=aT_ps[:].rearrange("p t q -> p q t"))
 
         STEPS = B * TILES
 
@@ -271,11 +272,13 @@ def tile_differentialattention_pa_t_kernel(
             load(0)
             for i in range(-TILES, STEPS + TILES):
                 b, quarter = divmod(i, TILES)
+                if is_step(i - 2):
+                    difference_transposed(i - 2)
                 if is_step(i + 2):
                     score_matmuls(i + 2)
                 if is_step(i - 1):
                     reciprocals(i - 1)
-                    scale_second(i - 1)
+                    normalise(i - 1)
                 if is_step(i + 1):
                     row_maxima(i + 1)
                 if is_step(i - 2):
@@ -307,5 +310,3 @@ def tile_differentialattention_pa_t_kernel(
                         output(b - 1, 1)
                     if is_batch(b + 1):
                         x_mx[b + 1] = quantise(x_mx[b + 1][:], S, "x")
-                if is_step(i - 1):
-                    difference_and_transpose(i - 1)

@@ -81,6 +81,7 @@ def tile_differentialattention_pa_t_kernel(
         a_pairs = {}
         scores = {}
         maxima = {}
+        shifts = {}
         exps = {}
         softmaxes = {}
         attn_T = {}
@@ -92,45 +93,35 @@ def tile_differentialattention_pa_t_kernel(
             nc.sync.dma_start(out=q_sb[:], in_=q[b].rearrange("(p j) d -> p j d", j=TILES))
             x_sb = loads.tile([P, TILES * D], BF16)
             nc.sync.dma_start(out=x_sb[:], in_=x[b].rearrange("(p t) d -> p (t d)", t=TILES))
-            loaded[b] = (x_sb, q_sb, k_sb)
+            loaded[b] = {"x": x_sb, "q": q_sb, "k": k_sb}
 
-        def transpose_qk(b):
-            x_sb, q_sb, k_sb = loaded[b]
-            transposed = []
-            for name, rows in (("kT", k_sb), ("qT", q_sb)):
-                t_ps = psum.tile([P, 2, TILES, P], BF16, name=name + "_ps", tag="aux", bufs=2)
-                for h in range(2):
-                    for j in range(TILES):
-                        nc.tensor.transpose(
-                            t_ps[:, h, j, :], rows[:, j, h * HD : (h + 1) * HD], ident_bf16[:]
-                        )
-                t_sb = batch.tile([P, 2, TILES, P], BF16, name=name, tag=name)
-                nc.scalar.copy(out=t_sb[:], in_=t_ps[:])
-                transposed.append(t_sb)
-            kT, qT = transposed
-            heads[b] = (qT, kT)
+        def transpose_head(b, name):
+            rows = loaded[b][name]
+            t_ps = psum.tile([P, 2, TILES, P], BF16, name=name + "_ps", tag="aux", bufs=2)
+            for h in range(2):
+                for j in range(TILES):
+                    nc.tensor.transpose(
+                        t_ps[:, h, j, :], rows[:, j, h * HD : (h + 1) * HD], ident_bf16[:]
+                    )
+            t_sb = batch.tile([P, 2, TILES, P], BF16, name=name, tag=name)
+            nc.scalar.copy(out=t_sb[:], in_=t_ps[:])
+            heads[(b, name)] = t_sb
 
-        def transpose_x(b):
-            x_sb, q_sb, k_sb = loaded.pop(b)
-            x_words = x_sb[:].bitcast(F32)
-            x_grouped = batch.tile([P, TILES * P * 4], BF16, align_bytes=64)
-            x_grouped_words = x_grouped[:].bitcast(F32).rearrange(
-                "p (t r g) -> p t r g", t=TILES, g=2
+        def transpose_x(b, pair):
+            x_words = loaded[b]["x"][:].bitcast(F32)
+            if pair == 0:
+                x_mx[b] = batch.tile([P, TILES * P * 4], BF16, name="x_grouped", align_bytes=64)
+            x_grouped_words = x_mx[b][:].bitcast(F32).rearrange("p (t r g) -> p t r g", t=TILES, g=2)
+            xT_ps = psum.tile([P, 2, 2, P], F32, tag="aux", bufs=2)
+            for i in range(2):
+                t = 2 * pair + i
+                for g in range(2):
+                    first = t * (D // 2) + g * P
+                    nc.tensor.transpose(xT_ps[:, i, g, :], x_words[:, first : first + P], ident_f32[:])
+            nc.scalar.copy(
+                out=x_grouped_words[:, 2 * pair : 2 * pair + 2, :, :],
+                in_=xT_ps[:].rearrange("p t g r -> p t r g"),
             )
-            for pair in range(TILES // 2):
-                xT_ps = psum.tile([P, 2, 2, P], F32, tag="aux", bufs=2)
-                for i in range(2):
-                    t = 2 * pair + i
-                    for g in range(2):
-                        first = t * (D // 2) + g * P
-                        nc.tensor.transpose(
-                            xT_ps[:, i, g, :], x_words[:, first : first + P], ident_f32[:]
-                        )
-                nc.scalar.copy(
-                    out=x_grouped_words[:, 2 * pair : 2 * pair + 2, :, :],
-                    in_=xT_ps[:].rearrange("p t g r -> p t r g"),
-                )
-            x_mx[b] = x_grouped
 
         def quantise(grouped, width, name):
             codes = batch.tile([P, width], U32, name=name + "_codes", align_bytes=64)
@@ -181,7 +172,7 @@ def tile_differentialattention_pa_t_kernel(
 
         def score_matmuls(step):
             b, j = divmod(step, TILES)
-            qT, kT = heads[b]
+            qT, kT = heads[(b, "q")], heads[(b, "k")]
             banks = []
             for h in range(2):
                 s_ps = psum.tile([P, S], F32, name="s_ps", tag="scores", bufs=4)
@@ -201,10 +192,16 @@ def tile_differentialattention_pa_t_kernel(
                 nc.vector.reduce_max(out=row_max[:, h : h + 1], in_=scores[step][h][:], axis=AXIS_X)
             maxima[step] = row_max
 
+        def exponent_shift(step):
+            shifts[step] = small.tile([P, 2], F32, name="shift")
+            nc.gpsimd.tensor_scalar(
+                out=shifts[step][:], in0=maxima.pop(step)[:], scalar1=-SCALE, scalar2=1.0,
+                op0=ALU.mult, op1=ALU.mult,
+            )
+
         def exponentials(step):
             banks = scores.pop(step)
-            shift = small.tile([P, 2], F32)
-            nc.vector.tensor_scalar_mul(out=shift[:], in0=maxima.pop(step)[:], scalar1=-SCALE)
+            shift = shifts.pop(step)
             expd = work.tile([P, 2, S], F32)
             row_sum = small.tile([P, 2], F32)
             for h in range(2):
@@ -237,20 +234,20 @@ def tile_differentialattention_pa_t_kernel(
             )
             softmaxes[step] = normed
 
-        def difference_transposed(step):
-            normed = softmaxes.pop(step)
-            aT_ps = psum.tile([P, TILES, P], F32, bufs=2)
+        def difference_transposed(step, h):
+            normed = softmaxes[step]
+            if h == 0:
+                attn_T[step] = psum.tile([P, TILES, P], F32, name="aT_ps", bufs=2)
+            aT_ps = attn_T[step]
             for t in range(TILES):
-                for h in range(2):
-                    nc.tensor.matmul(
-                        out=aT_ps[:, t, :],
-                        lhsT=normed[:, h, t * P : (t + 1) * P],
-                        rhs=ident_f32[:],
-                        start=(h == 0),
-                        stop=(h == 1),
-                        is_transpose=True,
-                    )
-            attn_T[step] = aT_ps
+                nc.tensor.matmul(
+                    out=aT_ps[:, t, :],
+                    lhsT=normed[:, h, t * P : (t + 1) * P],
+                    rhs=ident_f32[:],
+                    start=(h == 0 and t == 0),
+                    stop=(h == 1 and t == TILES - 1),
+                    is_transpose=True,
+                )
 
         def copy_attn(step):
             b, j = divmod(step, TILES)
@@ -269,44 +266,62 @@ def tile_differentialattention_pa_t_kernel(
             return 0 <= b < B
 
         with tc.manual_schedule():
-            load(0)
-            for i in range(-TILES, STEPS + TILES):
+            for i in range(-2 * TILES, STEPS + 2 * TILES):
                 b, quarter = divmod(i, TILES)
-                if is_step(i - 2):
-                    difference_transposed(i - 2)
-                if is_step(i + 2):
-                    score_matmuls(i + 2)
                 if is_step(i - 1):
                     reciprocals(i - 1)
+                if is_step(i - 1):
                     normalise(i - 1)
                 if is_step(i + 1):
                     row_maxima(i + 1)
-                if is_step(i - 2):
-                    copy_attn(i - 2)
+                if is_step(i + 1):
+                    exponent_shift(i + 1)
+                if is_step(i - 3):
+                    copy_attn(i - 3)
                 if is_step(i + 1):
                     exponentials(i + 1)
                 if quarter == 0:
                     if is_batch(b + 2):
                         load(b + 2)
+                if is_step(i - 2):
+                    difference_transposed(i - 2, 0)
+                if is_step(i - 2):
+                    difference_transposed(i - 2, 1)
+                if is_step(i + 2):
+                    score_matmuls(i + 2)
+                if quarter == 0:
                     if is_batch(b + 1):
-                        transpose_qk(b + 1)
-                    if is_batch(b - 1):
-                        a_pairs[(b - 1, 0)] = quantise(a_mx[b - 1][:, 0 : 2 * P * 4], 2 * P, "a")
+                        transpose_head(b + 1, "q")
                 if quarter == 1:
                     if is_batch(b + 1):
-                        transpose_x(b + 1)
+                        transpose_x(b + 1, 0)
+                if quarter == 2:
+                    if is_batch(b + 1):
+                        transpose_x(b + 1, 1)
+                if quarter == 3:
+                    if is_batch(b + 2):
+                        transpose_head(b + 2, "k")
+                if quarter == 0:
+                    if is_batch(b - 2):
+                        output(b - 2, 1)
+                if quarter == 1:
+                    if is_batch(b):
+                        project_v(b, 0)
+                if quarter == 2:
+                    if is_batch(b):
+                        project_v(b, 1)
+                if quarter == 3:
+                    if is_batch(b - 1):
+                        output(b - 1, 0)
+                if quarter == 0:
+                    if is_batch(b):
+                        x_mx[b] = quantise(x_mx[b][:], S, "x")
+                if quarter == 1:
                     if is_batch(b - 1):
                         v_mx[b - 1] = quantise(v_mx[b - 1][:].rearrange("p c t -> p (c t)"), HD2, "v")
                 if quarter == 2:
-                    if is_batch(b):
-                        project_v(b, 0)
                     if is_batch(b - 1):
-                        output(b - 1, 0)
-                        a_pairs[(b - 1, 1)] = quantise(a_mx[b - 1][:, 2 * P * 4 :], 2 * P, "a")
+                        a_pairs[(b - 1, 0)] = quantise(a_mx[b - 1][:, 0 : 2 * P * 4], 2 * P, "a")
                 if quarter == 3:
-                    if is_batch(b):
-                        project_v(b, 1)
                     if is_batch(b - 1):
-                        output(b - 1, 1)
-                    if is_batch(b + 1):
-                        x_mx[b + 1] = quantise(x_mx[b + 1][:], S, "x")
+                        a_pairs[(b - 1, 1)] = quantise(a_mx[b - 1][:, 2 * P * 4 :], 2 * P, "a")

@@ -73,6 +73,7 @@ def tile_differentialattention_pa_t_kernel(
             op0=ALU.add, op1=ALU.mult,
         )
 
+        aux = {}
         loaded = {}
         heads = {}
         x_mx = {}
@@ -80,8 +81,7 @@ def tile_differentialattention_pa_t_kernel(
         a_mx = {}
         a_pairs = {}
         scores = {}
-        maxima = {}
-        shifts = {}
+        negated = {}
         exps = {}
         softmaxes = {}
         attn_T = {}
@@ -97,30 +97,35 @@ def tile_differentialattention_pa_t_kernel(
 
         def transpose_head(b, name):
             rows = loaded[b][name]
-            t_ps = psum.tile([P, 2, TILES, P], BF16, name=name + "_ps", tag="aux", bufs=2)
+            t_ps = psum.tile([P, 2, TILES, P], BF16, name=name + "_ps", tag="aux", bufs=3)
             for h in range(2):
                 for j in range(TILES):
                     nc.tensor.transpose(
                         t_ps[:, h, j, :], rows[:, j, h * HD : (h + 1) * HD], ident_bf16[:]
                     )
-            t_sb = batch.tile([P, 2, TILES, P], BF16, name=name, tag=name)
-            nc.scalar.copy(out=t_sb[:], in_=t_ps[:])
-            heads[(b, name)] = t_sb
+            aux[(name, b)] = t_ps
+
+        def copy_head(b, name, copy):
+            heads[(b, name)] = batch.tile([P, 2, TILES, P], BF16, name=name, tag=name, bufs=3)
+            copy(out=heads[(b, name)][:], in_=aux.pop((name, b))[:])
 
         def transpose_x(b, pair):
             x_words = loaded[b]["x"][:].bitcast(F32)
-            if pair == 0:
-                x_mx[b] = batch.tile([P, TILES * P * 4], BF16, name="x_grouped", align_bytes=64)
-            x_grouped_words = x_mx[b][:].bitcast(F32).rearrange("p (t r g) -> p t r g", t=TILES, g=2)
-            xT_ps = psum.tile([P, 2, 2, P], F32, tag="aux", bufs=2)
+            xT_ps = psum.tile([P, 2, 2, P], F32, tag="aux", bufs=3)
             for i in range(2):
                 t = 2 * pair + i
                 for g in range(2):
                     first = t * (D // 2) + g * P
                     nc.tensor.transpose(xT_ps[:, i, g, :], x_words[:, first : first + P], ident_f32[:])
-            nc.scalar.copy(
+            aux[("x", b, pair)] = xT_ps
+
+        def copy_x(b, pair, copy):
+            if pair == 0:
+                x_mx[b] = batch.tile([P, TILES * P * 4], BF16, name="x_grouped", align_bytes=64)
+            x_grouped_words = x_mx[b][:].bitcast(F32).rearrange("p (t r g) -> p t r g", t=TILES, g=2)
+            copy(
                 out=x_grouped_words[:, 2 * pair : 2 * pair + 2, :, :],
-                in_=xT_ps[:].rearrange("p t g r -> p t r g"),
+                in_=aux.pop(("x", b, pair))[:].rearrange("p t g r -> p t r g"),
             )
 
         def quantise(grouped, width, name):
@@ -131,10 +136,8 @@ def tile_differentialattention_pa_t_kernel(
 
         def project_v(b, half):
             x_codes, x_scales = x_mx[b]
-            if half == 0:
-                v_mx[b] = batch.tile([P, HD2, TILES], BF16, name="v_grouped", align_bytes=64)
             cols = slice(half * P, (half + 1) * P)
-            v_ps = psum.tile([P, TILES, P], F32, tag="aux", bufs=2)
+            v_ps = psum.tile([P, TILES, P], F32, tag="aux", bufs=3)
             for t in range(TILES):
                 toks = slice(t * P, (t + 1) * P)
                 nc.tensor.matmul_mx(
@@ -146,14 +149,20 @@ def tile_differentialattention_pa_t_kernel(
                     start=True,
                     stop=True,
                 )
-            nc.scalar.copy(out=v_mx[b][:, cols, :], in_=v_ps[:].rearrange("p t c -> p c t"))
+            aux[("v", b, half)] = v_ps
+
+        def copy_v(b, half, copy):
+            if half == 0:
+                v_mx[b] = batch.tile([P, HD2, TILES], BF16, name="v_grouped", align_bytes=64)
+            cols = slice(half * P, (half + 1) * P)
+            copy(out=v_mx[b][:, cols, :], in_=aux.pop(("v", b, half))[:].rearrange("p t c -> p c t"))
 
         def output(b, pair):
-            a_codes, a_scales = a_pairs.pop((b, pair))
+            a_codes, a_scales = a_pairs[b]
             v_codes, v_scales = v_mx[b]
-            o_ps = psum.tile([P, 2, HD2], F32, tag="aux", bufs=2)
+            o_ps = psum.tile([P, 2, HD2], F32, tag="aux", bufs=3)
             for i in range(2):
-                rows = slice(i * P, (i + 1) * P)
+                rows = slice((2 * pair + i) * P, (2 * pair + i + 1) * P)
                 nc.tensor.matmul_mx(
                     out=o_ps[:, i, :],
                     lhsT=a_codes[:, rows].bitcast(FP8X4),
@@ -163,54 +172,50 @@ def tile_differentialattention_pa_t_kernel(
                     start=True,
                     stop=True,
                 )
+            aux[("o", b, pair)] = o_ps
+
+        def copy_output(b, pair, copy):
             out_sb = batch.tile([P, 2, HD2], F32)
-            nc.scalar.copy(out=out_sb[:], in_=o_ps[:])
+            copy(out=out_sb[:], in_=aux.pop(("o", b, pair))[:])
             nc.sync.dma_start(
                 out=out[b].rearrange("(p j) c -> p j c", j=TILES)[:, 2 * pair : 2 * pair + 2, :],
                 in_=out_sb[:],
             )
 
-        def score_matmuls(step):
+        def score_matmul(step, h):
             b, j = divmod(step, TILES)
             qT, kT = heads[(b, "q")], heads[(b, "k")]
-            banks = []
-            for h in range(2):
-                s_ps = psum.tile([P, S], F32, name="s_ps", tag="scores", bufs=4)
-                nc.tensor.matmul(
-                    out=s_ps[:],
-                    lhsT=qT[:, h, j, :],
-                    rhs=kT[:, h, :, :].rearrange("p m i -> p (m i)"),
-                    start=True,
-                    stop=True,
-                )
-                banks.append(s_ps)
-            scores[step] = banks
-
-        def row_maxima(step):
-            row_max = small.tile([P, 2], F32)
-            for h in range(2):
-                nc.vector.reduce_max(out=row_max[:, h : h + 1], in_=scores[step][h][:], axis=AXIS_X)
-            maxima[step] = row_max
-
-        def exponent_shift(step):
-            shifts[step] = small.tile([P, 2], F32, name="shift")
-            nc.gpsimd.tensor_scalar(
-                out=shifts[step][:], in0=maxima.pop(step)[:], scalar1=-SCALE, scalar2=1.0,
-                op0=ALU.mult, op1=ALU.mult,
+            s_ps = psum.tile([P, S], F32, name="s_ps", tag="scores", bufs=3)
+            nc.tensor.matmul(
+                out=s_ps[:],
+                lhsT=qT[:, h, j, :],
+                rhs=kT[:, h, :, :].rearrange("p m i -> p (m i)"),
+                start=True,
+                stop=True,
             )
+            scores[(step, h)] = s_ps
+
+        def negate_scores(step):
+            scaled = work.tile([P, 2, S], F32, bufs=3, name="scaled")
+            shift = small.tile([P, 2], F32, name="shift")
+            for h in range(2):
+                nc.vector.tensor_scalar(
+                    out=scaled[:, h, :], in0=scores.pop((step, h))[:], scalar1=-SCALE, scalar2=None,
+                    op0=ALU.mult, op1=ALU.min, accum_out=shift[:, h : h + 1],
+                )
+            negated[step] = (scaled, shift)
 
         def exponentials(step):
-            banks = scores.pop(step)
-            shift = shifts.pop(step)
-            expd = work.tile([P, 2, S], F32)
+            scaled, shift = negated.pop(step)
+            expd = work.tile([P, 2, S], F32, bufs=3)
             row_sum = small.tile([P, 2], F32)
             for h in range(2):
                 nc.scalar.activation(
                     out=expd[:, h, :],
-                    in_=banks[h][:],
+                    in_=scaled[:, h, :],
                     func=ACT.Exp,
                     bias=shift[:, h : h + 1],
-                    scale=SCALE,
+                    scale=-1.0,
                     accum_out=row_sum[:, h : h + 1],
                 )
             exps[step] = (expd, row_sum)
@@ -221,18 +226,14 @@ def tile_differentialattention_pa_t_kernel(
             nc.vector.reciprocal(out=inv_sum[:], in_=row_sum[:])
             exps[step] = (expd, inv_sum)
 
-        def normalise(step):
-            expd, inv_sum = exps.pop(step)
-            normed = work.tile([P, 2, S], F32)
+        def normalise(step, h):
+            expd, inv_sum = exps[step]
+            if h == 0:
+                softmaxes[step] = work.tile([P, 2, S], F32, bufs=3, name="normed")
             nc.gpsimd.tensor_scalar(
-                out=normed[:, 0, :], in0=expd[:, 0, :], scalar1=inv_sum[:, 0:1], scalar2=1.0,
-                op0=ALU.mult, op1=ALU.mult,
+                out=softmaxes[step][:, h, :], in0=expd[:, h, :], scalar1=inv_sum[:, h : h + 1],
+                scalar2=neg_lam[:, 0:1] if h == 1 else 1.0, op0=ALU.mult, op1=ALU.mult,
             )
-            nc.gpsimd.tensor_scalar(
-                out=normed[:, 1, :], in0=expd[:, 1, :], scalar1=inv_sum[:, 1:2],
-                scalar2=neg_lam[:, 0:1], op0=ALU.mult, op1=ALU.mult,
-            )
-            softmaxes[step] = normed
 
         def difference_transposed(step, h):
             normed = softmaxes[step]
@@ -266,62 +267,65 @@ def tile_differentialattention_pa_t_kernel(
             return 0 <= b < B
 
         with tc.manual_schedule():
-            for i in range(-2 * TILES, STEPS + 2 * TILES):
+            for i in range(-3 * TILES, STEPS + 3 * TILES):
                 b, quarter = divmod(i, TILES)
+                if quarter == 0 and is_batch(b + 2):
+                    load(b + 2)
+                if is_step(i + 0):
+                    exponentials(i + 0)
                 if is_step(i - 1):
                     reciprocals(i - 1)
                 if is_step(i - 1):
-                    normalise(i - 1)
-                if is_step(i + 1):
-                    row_maxima(i + 1)
-                if is_step(i + 1):
-                    exponent_shift(i + 1)
+                    normalise(i - 1, 0)
+                if is_step(i - 1):
+                    normalise(i - 1, 1)
                 if is_step(i - 3):
                     copy_attn(i - 3)
                 if is_step(i + 1):
-                    exponentials(i + 1)
-                if quarter == 0:
-                    if is_batch(b + 2):
-                        load(b + 2)
+                    negate_scores(i + 1)
                 if is_step(i - 2):
                     difference_transposed(i - 2, 0)
                 if is_step(i - 2):
                     difference_transposed(i - 2, 1)
+                if quarter == 3 and is_batch(b):
+                    project_v(b, 0)
+                if quarter == 3 and is_batch(b):
+                    project_v(b, 1)
+                if quarter == 0 and is_batch(b - 2):
+                    output(b - 2, 0)
+                if quarter == 0 and is_batch(b - 2):
+                    output(b - 2, 1)
+                if quarter == 3 and is_batch(b + 2):
+                    transpose_head(b + 2, "k")
+                if quarter == 0 and is_batch(b + 1):
+                    transpose_head(b + 1, "q")
+                if quarter == 1 and is_batch(b + 1):
+                    transpose_x(b + 1, 0)
+                if quarter == 2 and is_batch(b + 1):
+                    transpose_x(b + 1, 1)
                 if is_step(i + 2):
-                    score_matmuls(i + 2)
-                if quarter == 0:
-                    if is_batch(b + 1):
-                        transpose_head(b + 1, "q")
-                if quarter == 1:
-                    if is_batch(b + 1):
-                        transpose_x(b + 1, 0)
-                if quarter == 2:
-                    if is_batch(b + 1):
-                        transpose_x(b + 1, 1)
-                if quarter == 3:
-                    if is_batch(b + 2):
-                        transpose_head(b + 2, "k")
-                if quarter == 0:
-                    if is_batch(b - 2):
-                        output(b - 2, 1)
-                if quarter == 1:
-                    if is_batch(b):
-                        project_v(b, 0)
-                if quarter == 2:
-                    if is_batch(b):
-                        project_v(b, 1)
-                if quarter == 3:
-                    if is_batch(b - 1):
-                        output(b - 1, 0)
-                if quarter == 0:
-                    if is_batch(b):
-                        x_mx[b] = quantise(x_mx[b][:], S, "x")
-                if quarter == 1:
-                    if is_batch(b - 1):
-                        v_mx[b - 1] = quantise(v_mx[b - 1][:].rearrange("p c t -> p (c t)"), HD2, "v")
-                if quarter == 2:
-                    if is_batch(b - 1):
-                        a_pairs[(b - 1, 0)] = quantise(a_mx[b - 1][:, 0 : 2 * P * 4], 2 * P, "a")
-                if quarter == 3:
-                    if is_batch(b - 1):
-                        a_pairs[(b - 1, 1)] = quantise(a_mx[b - 1][:, 2 * P * 4 :], 2 * P, "a")
+                    score_matmul(i + 2, 0)
+                if is_step(i + 2):
+                    score_matmul(i + 2, 1)
+                if quarter == 3 and is_batch(b):
+                    copy_v(b, 0, nc.scalar.copy)
+                if quarter == 3 and is_batch(b):
+                    copy_v(b, 1, nc.scalar.copy)
+                if quarter == 0 and is_batch(b - 2):
+                    copy_output(b - 2, 0, nc.scalar.copy)
+                if quarter == 1 and is_batch(b - 2):
+                    copy_output(b - 2, 1, nc.scalar.copy)
+                if quarter == 3 and is_batch(b + 2):
+                    copy_head(b + 2, "k", nc.scalar.copy)
+                if quarter == 1 and is_batch(b + 1):
+                    copy_head(b + 1, "q", nc.scalar.copy)
+                if quarter == 2 and is_batch(b + 1):
+                    copy_x(b + 1, 0, nc.scalar.copy)
+                if quarter == 2 and is_batch(b + 1):
+                    copy_x(b + 1, 1, nc.scalar.copy)
+                if quarter == 0 and is_batch(b):
+                    x_mx[b] = quantise(x_mx[b][:], S, "x")
+                if quarter == 3 and is_batch(b - 1):
+                    v_mx[b - 1] = quantise(v_mx[b - 1][:].rearrange("p c t -> p (c t)"), HD2, "v")
+                if quarter == 3 and is_batch(b - 1):
+                    a_pairs[b - 1] = quantise(a_mx[b - 1][:], S, "a")

@@ -73,13 +73,15 @@ def tile_differentialattention_pa_t_kernel(
             op0=ALU.add, op1=ALU.mult,
         )
 
+        STEPS = B * TILES
+
         aux = {}
         loaded = {}
         heads = {}
         x_mx = {}
         v_mx = {}
         a_mx = {}
-        a_pairs = {}
+        a_tiles = {}
         scores = {}
         negated = {}
         exps = {}
@@ -134,6 +136,12 @@ def tile_differentialattention_pa_t_kernel(
             nc.vector.quantize_mx(out=codes[:].bitcast(FP8X4), scales=scales[:], in_=grouped)
             return codes, scales
 
+        def quantise_x(b):
+            x_mx[b] = quantise(x_mx[b][:], S, "x")
+
+        def quantise_v(b):
+            v_mx[b] = quantise(v_mx[b][:].rearrange("p c t -> p (c t)"), HD2, "v")
+
         def project_v(b, half):
             x_codes, x_scales = x_mx[b]
             cols = slice(half * P, (half + 1) * P)
@@ -157,29 +165,52 @@ def tile_differentialattention_pa_t_kernel(
             cols = slice(half * P, (half + 1) * P)
             copy(out=v_mx[b][:, cols, :], in_=aux.pop(("v", b, half))[:].rearrange("p t c -> p c t"))
 
-        def output(b, pair):
-            a_codes, a_scales = a_pairs[b]
+        def quantise_attn(b, first, tiles):
+            part = a_mx[b][:, first * P * 4 : (first + tiles) * P * 4]
+            for j, codes_scales in enumerate(split(quantise(part, tiles * P, "a%d" % tiles), tiles)):
+                a_tiles[(b, first + j)] = codes_scales
+
+        def split(codes_scales, tiles):
+            codes, scales = codes_scales
+            return [(codes[:, j * P : (j + 1) * P], scales[:, j * P : (j + 1) * P]) for j in range(tiles)]
+
+        def output(b, first, tiles):
             v_codes, v_scales = v_mx[b]
             o_ps = psum.tile([P, 2, HD2], F32, tag="aux", bufs=3)
-            for i in range(2):
-                rows = slice((2 * pair + i) * P, (2 * pair + i + 1) * P)
+            for i in range(tiles):
+                a_codes, a_scales = a_tiles.pop((b, first + i))
                 nc.tensor.matmul_mx(
                     out=o_ps[:, i, :],
-                    lhsT=a_codes[:, rows].bitcast(FP8X4),
-                    lhsT_scale=a_scales[:, rows],
+                    lhsT=a_codes.bitcast(FP8X4),
+                    lhsT_scale=a_scales,
                     rhs=v_codes[:].bitcast(FP8X4),
                     rhs_scale=v_scales[:],
                     start=True,
                     stop=True,
                 )
-            aux[("o", b, pair)] = o_ps
+            aux[("o", b, first)] = o_ps
 
-        def copy_output(b, pair, copy):
-            out_sb = batch.tile([P, 2, HD2], F32)
-            copy(out=out_sb[:], in_=aux.pop(("o", b, pair))[:])
+        def copy_output(b, first, tiles, copy):
+            out_sb = batch.tile([P, 2, HD2], F32, bufs=4)
+            copy(out=out_sb[:, 0:tiles, :], in_=aux.pop(("o", b, first))[:, 0:tiles, :])
             nc.sync.dma_start(
-                out=out[b].rearrange("(p j) c -> p j c", j=TILES)[:, 2 * pair : 2 * pair + 2, :],
-                in_=out_sb[:],
+                out=out[b].rearrange("(p j) c -> p j c", j=TILES)[:, first : first + tiles, :],
+                in_=out_sb[:, 0:tiles, :],
+            )
+
+        def warm_up(n):
+            warm_ps = psum.tile([P, TILES, P], F32, tag="aux", bufs=3)
+            for i in range(n):
+                nc.tensor.matmul(
+                    out=warm_ps[:, 0, :], lhsT=ident_bf16[:], rhs=ident_bf16[:], start=True, stop=True
+                )
+
+        def keep_warm():
+            s_ps = psum.tile([P, S], F32, name="s_ps", tag="scores", bufs=3)
+            kT = heads[(B - 1, "k")]
+            nc.tensor.matmul(
+                out=s_ps[:], lhsT=ident_bf16[:], rhs=kT[:, 0, :, :].rearrange("p m i -> p (m i)"),
+                start=True, stop=True,
             )
 
         def score_matmul(step, h):
@@ -196,7 +227,7 @@ def tile_differentialattention_pa_t_kernel(
             scores[(step, h)] = s_ps
 
         def negate_scores(step):
-            scaled = work.tile([P, 2, S], F32, bufs=3, name="scaled")
+            scaled = work.tile([P, 2, S], F32, bufs=4, name="scaled")
             shift = small.tile([P, 2], F32, name="shift")
             for h in range(2):
                 nc.vector.tensor_scalar(
@@ -207,7 +238,7 @@ def tile_differentialattention_pa_t_kernel(
 
         def exponentials(step):
             scaled, shift = negated.pop(step)
-            expd = work.tile([P, 2, S], F32, bufs=3)
+            expd = work.tile([P, 2, S], F32, bufs=4)
             row_sum = small.tile([P, 2], F32)
             for h in range(2):
                 nc.scalar.activation(
@@ -229,8 +260,9 @@ def tile_differentialattention_pa_t_kernel(
         def normalise(step, h):
             expd, inv_sum = exps[step]
             if h == 0:
-                softmaxes[step] = work.tile([P, 2, S], F32, bufs=3, name="normed")
-            nc.gpsimd.tensor_scalar(
+                softmaxes[step] = work.tile([P, 2, S], F32, bufs=4, name="normed")
+            engine = nc.vector if step == STEPS - 1 else nc.gpsimd
+            engine.tensor_scalar(
                 out=softmaxes[step][:, h, :], in0=expd[:, h, :], scalar1=inv_sum[:, h : h + 1],
                 scalar2=neg_lam[:, 0:1] if h == 1 else 1.0, op0=ALU.mult, op1=ALU.mult,
             )
@@ -250,82 +282,66 @@ def tile_differentialattention_pa_t_kernel(
                     is_transpose=True,
                 )
 
-        def copy_attn(step):
+        def copy_attn(step, copy):
             b, j = divmod(step, TILES)
             if j == 0:
                 a_mx[b] = batch.tile([P, TILES * P * 4], BF16, name="a_grouped", align_bytes=64)
             a_grouped = a_mx[b][:].rearrange("p (j q t) -> p j q t", j=TILES, t=TILES)
             aT_ps = attn_T.pop(step)
-            nc.vector.tensor_copy(out=a_grouped[:, j, :, :], in_=aT_ps[:].rearrange("p t q -> p q t"))
+            copy(out=a_grouped[:, j, :, :], in_=aT_ps[:].rearrange("p t q -> p q t"))
 
-        STEPS = B * TILES
+        SV = (nc.scalar.copy, nc.vector.tensor_copy)
+        plan = {}
 
-        def is_step(step):
-            return 0 <= step < STEPS
+        def at(rnd, slot, stage, *args):
+            plan.setdefault((rnd, slot), []).append((stage, args))
 
-        def is_batch(b):
-            return 0 <= b < B
+        at(-9, "warm", warm_up, 16)
+        for b in range(B):
+            r = TILES * b
+            first, last = b == 0, b == B - 1
+            at(r - 8, "load", load, b)
+            k_round = r + (-5) + (0 if b == 1 else 0)
+            q_round = r + (-4) + (0 if b == 1 else 0)
+            at(k_round, "transpose", transpose_head, b, "k")
+            at(k_round, "copy T", copy_head, b, "k", SV[0])
+            at(q_round, "transpose", transpose_head, b, "q")
+            at(q_round + (1 if b != 1 else 0), "copy T", copy_head, b, "q", SV[0])
+            for pair in range(2):
+                x_round = (-3 + pair if first else r + ((-3) if pair == 0 else (-2)))
+                at(x_round, "transpose", transpose_x, b, pair)
+                at(x_round + 1 * (1 - pair), "copy T", copy_x, b, pair, SV[0])
+                v_round = r + (2 if last else (3) if pair == 0 else (3))
+                at(v_round, "mx", project_v, b, pair)
+                at(v_round, "copy MX", copy_v, b, pair, SV[0])
+                if not last:
+                    at(r + (8), "mx", output, b, 2 * pair, 2)
+                    at(r + (8) + (1) * pair, "copy MX", copy_output, b, 2 * pair, 2, SV[0])
+            at(r + (0 if first else 0), "quantise", quantise_x, b)
+            at(r + (4 if last else 7), "quantise", quantise_v, b)
+            if not last:
+                at(r + (7), "quantise", quantise_attn, b, 0, TILES)
+        for s in range(STEPS):
+            at(s - 2, "score 0", score_matmul, s, 0)
+            at(s - 2, "score 1", score_matmul, s, 1)
+            at(s - 1, "negate", negate_scores, s)
+            at(s, "exp", exponentials, s)
+            at(s + 1, "reciprocal", reciprocals, s)
+            for h in range(2):
+                at(s + 1, "normalise", normalise, s, h)
+                at(s + 2, "attn " + str(h), difference_transposed, s, h)
+            at(s + 3, "copy attn", copy_attn, s, SV[0] if False else SV[1])
+        for rnd, first, tiles in ((STEPS + 2, 0, 2), (STEPS + 3, 2, 1), (STEPS + 4, 3, 1)):
+            at(rnd, "tail", quantise_attn, B - 1, first, tiles)
+            at(rnd, "tail", output, B - 1, first, tiles)
+            at(rnd, "tail", copy_output, B - 1, first, tiles, SV[0])
+        for i in range(4):
+            at(STEPS - 2 + i, "score 0", keep_warm)
+            at(STEPS - 2 + i, "score 1", keep_warm)
 
+        ORDER = ("warm", "load", "exp", "reciprocal", "normalise", "copy attn", "negate", "attn 0", "attn 1", "mx", "transpose", "score 0", "score 1", "copy MX", "copy T", "quantise", "tail")
         with tc.manual_schedule():
-            for i in range(-3 * TILES, STEPS + 3 * TILES):
-                b, quarter = divmod(i, TILES)
-                if quarter == 0 and is_batch(b + 2):
-                    load(b + 2)
-                if is_step(i + 0):
-                    exponentials(i + 0)
-                if is_step(i - 1):
-                    reciprocals(i - 1)
-                if is_step(i - 1):
-                    normalise(i - 1, 0)
-                if is_step(i - 1):
-                    normalise(i - 1, 1)
-                if is_step(i - 3):
-                    copy_attn(i - 3)
-                if is_step(i + 1):
-                    negate_scores(i + 1)
-                if is_step(i - 2):
-                    difference_transposed(i - 2, 0)
-                if is_step(i - 2):
-                    difference_transposed(i - 2, 1)
-                if quarter == 3 and is_batch(b):
-                    project_v(b, 0)
-                if quarter == 3 and is_batch(b):
-                    project_v(b, 1)
-                if quarter == 0 and is_batch(b - 2):
-                    output(b - 2, 0)
-                if quarter == 0 and is_batch(b - 2):
-                    output(b - 2, 1)
-                if quarter == 3 and is_batch(b + 2):
-                    transpose_head(b + 2, "k")
-                if quarter == 0 and is_batch(b + 1):
-                    transpose_head(b + 1, "q")
-                if quarter == 1 and is_batch(b + 1):
-                    transpose_x(b + 1, 0)
-                if quarter == 2 and is_batch(b + 1):
-                    transpose_x(b + 1, 1)
-                if is_step(i + 2):
-                    score_matmul(i + 2, 0)
-                if is_step(i + 2):
-                    score_matmul(i + 2, 1)
-                if quarter == 3 and is_batch(b):
-                    copy_v(b, 0, nc.scalar.copy)
-                if quarter == 3 and is_batch(b):
-                    copy_v(b, 1, nc.scalar.copy)
-                if quarter == 0 and is_batch(b - 2):
-                    copy_output(b - 2, 0, nc.scalar.copy)
-                if quarter == 1 and is_batch(b - 2):
-                    copy_output(b - 2, 1, nc.scalar.copy)
-                if quarter == 3 and is_batch(b + 2):
-                    copy_head(b + 2, "k", nc.scalar.copy)
-                if quarter == 1 and is_batch(b + 1):
-                    copy_head(b + 1, "q", nc.scalar.copy)
-                if quarter == 2 and is_batch(b + 1):
-                    copy_x(b + 1, 0, nc.scalar.copy)
-                if quarter == 2 and is_batch(b + 1):
-                    copy_x(b + 1, 1, nc.scalar.copy)
-                if quarter == 0 and is_batch(b):
-                    x_mx[b] = quantise(x_mx[b][:], S, "x")
-                if quarter == 3 and is_batch(b - 1):
-                    v_mx[b - 1] = quantise(v_mx[b - 1][:].rearrange("p c t -> p (c t)"), HD2, "v")
-                if quarter == 3 and is_batch(b - 1):
-                    a_pairs[b - 1] = quantise(a_mx[b - 1][:], S, "a")
+            for i in range(-9, STEPS + 10):
+                for slot in ORDER:
+                    for stage, args in plan.get((i, slot), []):
+                        stage(*args)

@@ -109,7 +109,10 @@ def tile_differentialattention_pa_t_kernel(
 
         def copy_head(b, name, copy):
             heads[(b, name)] = batch.tile([P, 2, TILES, P], BF16, name=name, tag=name, bufs=3)
-            copy(out=heads[(b, name)][:], in_=aux.pop((name, b))[:])
+            copy(
+                out=heads[(b, name)][:].rearrange("p h j i -> p (h j i)").bitcast(F32),
+                in_=aux.pop((name, b))[:].rearrange("p h j i -> p (h j i)").bitcast(F32),
+            )
 
         def transpose_x(b, pair):
             x_words = loaded[b]["x"][:].bitcast(F32)
@@ -261,7 +264,7 @@ def tile_differentialattention_pa_t_kernel(
             expd, inv_sum = exps[step]
             if h == 0:
                 softmaxes[step] = work.tile([P, 2, S], F32, bufs=4, name="normed")
-            engine = nc.vector if step == STEPS - 1 else nc.gpsimd
+            engine = nc.vector if step >= STEPS - 0 else nc.gpsimd
             engine.tensor_scalar(
                 out=softmaxes[step][:, h, :], in0=expd[:, h, :], scalar1=inv_sum[:, h : h + 1],
                 scalar2=neg_lam[:, 0:1] if h == 1 else 1.0, op0=ALU.mult, op1=ALU.mult,
@@ -299,28 +302,30 @@ def tile_differentialattention_pa_t_kernel(
         at(-9, "warm", warm_up, 16)
         for b in range(B):
             r = TILES * b
-            first, last = b == 0, b == B - 1
+            last = b == B - 1
             at(r - 8, "load", load, b)
-            k_round = r + (-5) + (0 if b == 1 else 0)
-            q_round = r + (-4) + (0 if b == 1 else 0)
-            at(k_round, "transpose", transpose_head, b, "k")
-            at(k_round, "copy T", copy_head, b, "k", SV[0])
-            at(q_round, "transpose", transpose_head, b, "q")
-            at(q_round + (1 if b != 1 else 0), "copy T", copy_head, b, "q", SV[0])
-            for pair in range(2):
-                x_round = (-3 + pair if first else r + ((-3) if pair == 0 else (-2)))
-                at(x_round, "transpose", transpose_x, b, pair)
-                at(x_round + 1 * (1 - pair), "copy T", copy_x, b, pair, SV[0])
-                v_round = r + (2 if last else (3) if pair == 0 else (3))
-                at(v_round, "mx", project_v, b, pair)
-                at(v_round, "copy MX", copy_v, b, pair, SV[0])
-                if not last:
-                    at(r + (8), "mx", output, b, 2 * pair, 2)
-                    at(r + (8) + (1) * pair, "copy MX", copy_output, b, 2 * pair, 2, SV[0])
-            at(r + (0 if first else 0), "quantise", quantise_x, b)
-            at(r + (4 if last else 7), "quantise", quantise_v, b)
+            at(r + (-5), "transpose", transpose_head, b, "k")
+            at(r + (-5), "copy T", copy_head, b, "k", SV[0])
+            at(r + (-4), "transpose", transpose_head, b, "q")
+            at(r + (-3), "copy T", copy_head, b, "q", SV[0])
+            at(r + (-3), "transpose", transpose_x, b, 0)
+            at(r + (-3), "copy T", copy_x, b, 0, SV[0])
+            at(r + (-2), "transpose", transpose_x, b, 1)
+            at(r + (-2), "copy T", copy_x, b, 1, SV[0])
+            at(r + (1 if last else 3), "mx v", project_v, b, 0)
+            at(r + (1 if last else 3), "copy V", copy_v, b, 0, SV[0])
+            at(r + (1 if last else 3), "mx v", project_v, b, 1)
+            at(r + (1 if last else 3), "copy V", copy_v, b, 1, SV[0])
             if not last:
-                at(r + (7), "quantise", quantise_attn, b, 0, TILES)
+                at(r + (8), "mx o", output, b, 2 * 0, 2)
+                at(r + (8), "copy O", copy_output, b, 2 * 0, 2, SV[0])
+            if not last:
+                at(r + (8), "mx o", output, b, 2 * 1, 2)
+                at(r + (9), "copy O", copy_output, b, 2 * 1, 2, SV[0])
+            at(r + (-1), "quantise x", quantise_x, b)
+            at(r + (3 if last else 5), "quantise v", quantise_v, b)
+            if not last:
+                at(r + (7), "quantise a", quantise_attn, b, 0, TILES)
         for s in range(STEPS):
             at(s - 2, "score 0", score_matmul, s, 0)
             at(s - 2, "score 1", score_matmul, s, 1)
@@ -329,7 +334,7 @@ def tile_differentialattention_pa_t_kernel(
             at(s + 1, "reciprocal", reciprocals, s)
             for h in range(2):
                 at(s + 1, "normalise", normalise, s, h)
-                at(s + 2, "attn " + str(h), difference_transposed, s, h)
+                at(s + 2, "attn", difference_transposed, s, h)
             at(s + 3, "copy attn", copy_attn, s, SV[0] if False else SV[1])
         for rnd, first, tiles in ((STEPS + 2, 0, 2), (STEPS + 3, 2, 1), (STEPS + 4, 3, 1)):
             at(rnd, "tail", quantise_attn, B - 1, first, tiles)
@@ -338,8 +343,7 @@ def tile_differentialattention_pa_t_kernel(
         for i in range(4):
             at(STEPS - 2 + i, "score 0", keep_warm)
             at(STEPS - 2 + i, "score 1", keep_warm)
-
-        ORDER = ("warm", "load", "exp", "reciprocal", "normalise", "copy attn", "negate", "attn 0", "attn 1", "mx", "transpose", "score 0", "score 1", "copy MX", "copy T", "quantise", "tail")
+        ORDER = ("warm", "load", "quantise v", "reciprocal", "quantise a", "mx o", "exp", "mx v", "copy V", "tail", "transpose", "score 0", "copy attn", "attn", "copy O", "negate", "copy T", "quantise x", "score 1", "normalise")
         with tc.manual_schedule():
             for i in range(-9, STEPS + 10):
                 for slot in ORDER:

@@ -230,7 +230,7 @@ def tile_differentialattention_pa_t_kernel(
             scores[(step, h)] = s_ps
 
         def negate_scores(step):
-            scaled = work.tile([P, 2, S], F32, bufs=4, name="scaled")
+            scaled = work.tile([P, 2, S], F32, bufs=5, name="scaled")
             shift = small.tile([P, 2], F32, name="shift")
             for h in range(2):
                 nc.vector.tensor_scalar(
@@ -241,7 +241,7 @@ def tile_differentialattention_pa_t_kernel(
 
         def exponentials(step):
             scaled, shift = negated.pop(step)
-            expd = work.tile([P, 2, S], F32, bufs=4)
+            expd = work.tile([P, 2, S], F32, bufs=5)
             row_sum = small.tile([P, 2], F32)
             for h in range(2):
                 nc.scalar.activation(
@@ -263,8 +263,8 @@ def tile_differentialattention_pa_t_kernel(
         def normalise(step, h):
             expd, inv_sum = exps[step]
             if h == 0:
-                softmaxes[step] = work.tile([P, 2, S], F32, bufs=4, name="normed")
-            engine = nc.vector if step >= STEPS - 0 else nc.gpsimd
+                softmaxes[step] = work.tile([P, 2, S], F32, bufs=5, name="normed")
+            engine = nc.vector if step >= STEPS - 2 else nc.gpsimd
             engine.tensor_scalar(
                 out=softmaxes[step][:, h, :], in0=expd[:, h, :], scalar1=inv_sum[:, h : h + 1],
                 scalar2=neg_lam[:, 0:1] if h == 1 else 1.0, op0=ALU.mult, op1=ALU.mult,
@@ -309,13 +309,13 @@ def tile_differentialattention_pa_t_kernel(
             at(r + (-4), "transpose", transpose_head, b, "q")
             at(r + (-3), "copy T", copy_head, b, "q", SV[0])
             at(r + (-3), "transpose", transpose_x, b, 0)
-            at(r + (-3), "copy T", copy_x, b, 0, SV[0])
+            at(r + (-2), "copy T", copy_x, b, 0, SV[0])
             at(r + (-2), "transpose", transpose_x, b, 1)
             at(r + (-2), "copy T", copy_x, b, 1, SV[0])
-            at(r + (1 if last else 3), "mx v", project_v, b, 0)
-            at(r + (1 if last else 3), "copy V", copy_v, b, 0, SV[0])
-            at(r + (1 if last else 3), "mx v", project_v, b, 1)
-            at(r + (1 if last else 3), "copy V", copy_v, b, 1, SV[0])
+            at(r + (2 if last else 3), "mx v", project_v, b, 0)
+            at(r + (2 if last else 3), "copy V", copy_v, b, 0, SV[0])
+            at(r + (2 if last else 3), "mx v", project_v, b, 1)
+            at(r + (2 if last else 3), "copy V", copy_v, b, 1, SV[0])
             if not last:
                 at(r + (8), "mx o", output, b, 2 * 0, 2)
                 at(r + (8), "copy O", copy_output, b, 2 * 0, 2, SV[0])
@@ -323,7 +323,7 @@ def tile_differentialattention_pa_t_kernel(
                 at(r + (8), "mx o", output, b, 2 * 1, 2)
                 at(r + (9), "copy O", copy_output, b, 2 * 1, 2, SV[0])
             at(r + (-1), "quantise x", quantise_x, b)
-            at(r + (3 if last else 5), "quantise v", quantise_v, b)
+            at(r + (5 if last else 6), "quantise v", quantise_v, b)
             if not last:
                 at(r + (7), "quantise a", quantise_attn, b, 0, TILES)
         for s in range(STEPS):
@@ -343,7 +343,7 @@ def tile_differentialattention_pa_t_kernel(
         for i in range(4):
             at(STEPS - 2 + i, "score 0", keep_warm)
             at(STEPS - 2 + i, "score 1", keep_warm)
-        ORDER = ("warm", "load", "quantise v", "reciprocal", "quantise a", "mx o", "exp", "mx v", "copy V", "tail", "transpose", "score 0", "copy attn", "attn", "copy O", "negate", "copy T", "quantise x", "score 1", "normalise")
+        ORDER = ("load", "exp", "tail", "reciprocal", "attn", "copy attn", "negate", "mx o", "mx v", "normalise", "transpose", "quantise a", "quantise x", "score 0", "warm", "score 1", "copy V", "copy T", "quantise v", "copy O")
         with tc.manual_schedule():
             for i in range(-9, STEPS + 10):
                 for slot in ORDER:

import math
from contextlib import ExitStack

import concourse.mybir as mybir
from concourse.masks import make_identity

F32 = mybir.dt.float32
BF16 = mybir.dt.bfloat16
U32 = mybir.dt.uint32
U8 = mybir.dt.uint8
FP8X4 = mybir.dt.float8_e4m3fn_x4
ALU = mybir.AluOpType
ACT = mybir.ActivationFunctionType
AXIS_X = mybir.AxisListType.X

P = 128
B, S, D, HD = 16, 512, 512, 128
HD2 = 2 * HD
TILES = S // P
SCALE = HD**-0.5
LAMBDA_INIT = 0.8 - 0.6 * math.exp(-0.3 * 12)

FLOPS = B * (2 * S * D * HD2 + 2 * 2 * S * S * HD + 2 * S * S * HD2)


def tile_differentialattention_pa_t_kernel(
    tc, x, q, k, WV, lambda_q1, lambda_q2, lambda_k1, lambda_k2, out
):
    nc = tc.nc
    with ExitStack() as stack:
        const = stack.enter_context(tc.tile_pool(name="const", bufs=1))
        loads = stack.enter_context(tc.tile_pool(name="loads", bufs=3))
        batch = stack.enter_context(tc.tile_pool(name="batch", bufs=2))
        work = stack.enter_context(tc.tile_pool(name="work", bufs=3))
        small = stack.enter_context(tc.tile_pool(name="small", bufs=4))
        psum = stack.enter_context(tc.psum_pool(name="psum", bufs=2))

        ident_bf16 = const.tile([P, P], BF16)
        make_identity(nc, ident_bf16[:])
        ident_f32 = const.tile([P, P], F32)
        make_identity(nc, ident_f32[:])

        wv_rows = const.tile([P, 4, HD2], BF16)
        nc.scalar.dma_start(
            out=wv_rows[:].rearrange("p (g e) c -> p g (e c)", g=2),
            in_=WV.rearrange("(g p e) c -> p g (e c)", g=2, e=2),
        )
        wv_grouped = const.tile([P, HD2, 4], BF16, align_bytes=64)
        nc.vector.tensor_copy(out=wv_grouped[:], in_=wv_rows[:].rearrange("p t c -> p c t"))
        wv_codes = const.tile([P, HD2], U32, align_bytes=64)
        wv_scales = const.tile([P, HD2], U8, align_bytes=64)
        nc.vector.quantize_mx(
            out=wv_codes[:].bitcast(FP8X4),
            scales=wv_scales[:],
            in_=wv_grouped[:].rearrange("p c t -> p (c t)"),
        )

        lam_vecs = const.tile([P, 4, HD], BF16)
        for i, vec in enumerate((lambda_q1, lambda_q2, lambda_k1, lambda_k2)):
            nc.scalar.dma_start(out=lam_vecs[:, i, :], in_=vec.partition_broadcast(P))
        lam_prod = const.tile([P, 2, HD], F32)
        nc.vector.tensor_tensor(
            out=lam_prod[:], in0=lam_vecs[:, 0:2, :], in1=lam_vecs[:, 2:4, :], op=ALU.mult
        )
        lam_dots = const.tile([P, 2], F32)
        nc.vector.reduce_sum(out=lam_dots[:], in_=lam_prod[:], axis=AXIS_X)
        lam_exps = const.tile([P, 2], F32)
        lam_sum = const.tile([P, 1], F32)
        nc.scalar.activation(out=lam_exps[:], in_=lam_dots[:], func=ACT.Exp, accum_out=lam_sum[:])
        neg_lam = const.tile([P, 1], F32)
        nc.vector.tensor_scalar(
            out=neg_lam[:], in0=lam_sum[:], scalar1=LAMBDA_INIT, scalar2=-1.0,
            op0=ALU.add, op1=ALU.mult,
        )

        STEPS = B * TILES

        aux = {}
        loaded = {}
        heads = {}
        x_mx = {}
        v_mx = {}
        a_mx = {}
        a_tiles = {}
        scores = {}
        negated = {}
        exps = {}
        softmaxes = {}
        attn_T = {}

        def load(b):
            k_sb = loads.tile([P, TILES, HD2], BF16)
            nc.sync.dma_start(out=k_sb[:], in_=k[b].rearrange("(p t) d -> p t d", t=TILES))
            q_sb = loads.tile([P, TILES, HD2], BF16)
            nc.sync.dma_start(out=q_sb[:], in_=q[b].rearrange("(p j) d -> p j d", j=TILES))
            x_sb = loads.tile([P, TILES * D], BF16)
            nc.sync.dma_start(out=x_sb[:], in_=x[b].rearrange("(p t) d -> p (t d)", t=TILES))
            loaded[b] = {"x": x_sb, "q": q_sb, "k": k_sb}

        def transpose_head(b, name):
            rows = loaded[b][name]
            t_ps = psum.tile([P, 2, TILES, P], BF16, name=name + "_ps", tag="aux", bufs=3)
            for h in range(2):
                for j in range(TILES):
                    nc.tensor.transpose(
                        t_ps[:, h, j, :], rows[:, j, h * HD : (h + 1) * HD], ident_bf16[:]
                    )
            aux[(name, b)] = t_ps

        def copy_head(b, name, copy):
            heads[(b, name)] = batch.tile([P, 2, TILES, P], BF16, name=name, tag=name, bufs=3)
            copy(
                out=heads[(b, name)][:].rearrange("p h j i -> p (h j i)").bitcast(F32),
                in_=aux.pop((name, b))[:].rearrange("p h j i -> p (h j i)").bitcast(F32),
            )

        def transpose_x(b, pair):
            x_words = loaded[b]["x"][:].bitcast(F32)
            xT_ps = psum.tile([P, 2, 2, P], F32, tag="aux", bufs=3)
            for i in range(2):
                t = 2 * pair + i
                for g in range(2):
                    first = t * (D // 2) + g * P
                    nc.tensor.transpose(xT_ps[:, i, g, :], x_words[:, first : first + P], ident_f32[:])
            aux[("x", b, pair)] = xT_ps

        def copy_x(b, pair, copy):
            if pair == 0:
                x_mx[b] = batch.tile([P, TILES * P * 4], BF16, name="x_grouped", align_bytes=64)
            x_grouped_words = x_mx[b][:].bitcast(F32).rearrange("p (t r g) -> p t r g", t=TILES, g=2)
            copy(
                out=x_grouped_words[:, 2 * pair : 2 * pair + 2, :, :],
                in_=aux.pop(("x", b, pair))[:].rearrange("p t g r -> p t r g"),
            )

        def quantise(grouped, width, name):
            codes = batch.tile([P, width], U32, name=name + "_codes", align_bytes=64)
            scales = batch.tile([P, width], U8, name=name + "_scales", align_bytes=64)
            nc.vector.quantize_mx(out=codes[:].bitcast(FP8X4), scales=scales[:], in_=grouped)
            return codes, scales

        def quantise_x(b):
            x_mx[b] = quantise(x_mx[b][:], S, "x")

        def quantise_v(b):
            v_mx[b] = quantise(v_mx[b][:].rearrange("p c t -> p (c t)"), HD2, "v")

        def project_v(b, half):
            x_codes, x_scales = x_mx[b]
            cols = slice(half * P, (half + 1) * P)
            v_ps = psum.tile([P, TILES, P], F32, tag="aux", bufs=3)
            for t in range(TILES):
                toks = slice(t * P, (t + 1) * P)
                nc.tensor.matmul_mx(
                    out=v_ps[:, t, :],
                    lhsT=x_codes[:, toks].bitcast(FP8X4),
                    lhsT_scale=x_scales[:, toks],
                    rhs=wv_codes[:, cols].bitcast(FP8X4),
                    rhs_scale=wv_scales[:, cols],
                    start=True,
                    stop=True,
                )
            aux[("v", b, half)] = v_ps

        def copy_v(b, half, copy):
            if half == 0:
                v_mx[b] = batch.tile([P, HD2, TILES], BF16, name="v_grouped", align_bytes=64)
            cols = slice(half * P, (half + 1) * P)
            copy(out=v_mx[b][:, cols, :], in_=aux.pop(("v", b, half))[:].rearrange("p t c -> p c t"))

        def quantise_attn(b, first, tiles):
            part = a_mx[b][:, first * P * 4 : (first + tiles) * P * 4]
            for j, codes_scales in enumerate(split(quantise(part, tiles * P, "a%d" % tiles), tiles)):
                a_tiles[(b, first + j)] = codes_scales

        def split(codes_scales, tiles):
            codes, scales = codes_scales
            return [(codes[:, j * P : (j + 1) * P], scales[:, j * P : (j + 1) * P]) for j in range(tiles)]

        def output(b, first, tiles):
            v_codes, v_scales = v_mx[b]
            o_ps = psum.tile([P, 2, HD2], F32, tag="aux", bufs=3)
            for i in range(tiles):
                a_codes, a_scales = a_tiles.pop((b, first + i))
                nc.tensor.matmul_mx(
                    out=o_ps[:, i, :],
                    lhsT=a_codes.bitcast(FP8X4),
                    lhsT_scale=a_scales,
                    rhs=v_codes[:].bitcast(FP8X4),
                    rhs_scale=v_scales[:],
                    start=True,
                    stop=True,
                )
            aux[("o", b, first)] = o_ps

        def copy_output(b, first, tiles, copy):
            out_sb = batch.tile([P, 2, HD2], F32, bufs=4)
            copy(out=out_sb[:, 0:tiles, :], in_=aux.pop(("o", b, first))[:, 0:tiles, :])
            nc.sync.dma_start(
                out=out[b].rearrange("(p j) c -> p j c", j=TILES)[:, first : first + tiles, :],
                in_=out_sb[:, 0:tiles, :],
            )

        def warm_up(n):
            warm_ps = psum.tile([P, TILES, P], F32, tag="aux", bufs=3)
            for i in range(n):
                nc.tensor.matmul(
                    out=warm_ps[:, 0, :], lhsT=ident_bf16[:], rhs=ident_bf16[:], start=True, stop=True
                )

        def keep_warm():
            s_ps = psum.tile([P, S], F32, name="s_ps", tag="scores", bufs=3)
            kT = heads[(B - 1, "k")]
            nc.tensor.matmul(
                out=s_ps[:], lhsT=ident_bf16[:], rhs=kT[:, 0, :, :].rearrange("p m i -> p (m i)"),
                start=True, stop=True,
            )

        def score_matmul(step, h):
            b, j = divmod(step, TILES)
            qT, kT = heads[(b, "q")], heads[(b, "k")]
            s_ps = psum.tile([P, S], F32, name="s_ps", tag="scores", bufs=3)
            nc.tensor.matmul(
                out=s_ps[:],
                lhsT=qT[:, h, j, :],
                rhs=kT[:, h, :, :].rearrange("p m i -> p (m i)"),
                start=True,
                stop=True,
            )
            scores[(step, h)] = s_ps

        def negate_scores(step):
            scaled = work.tile([P, 2, S], F32, bufs=5, name="scaled")
            shift = small.tile([P, 2], F32, name="shift")
            for h in range(2):
                nc.vector.tensor_scalar(
                    out=scaled[:, h, :], in0=scores.pop((step, h))[:], scalar1=-SCALE, scalar2=None,
                    op0=ALU.mult, op1=ALU.min, accum_out=shift[:, h : h + 1],
                )
            negated[step] = (scaled, shift)

        def exponentials(step):
            scaled, shift = negated.pop(step)
            expd = work.tile([P, 2, S], F32, bufs=5)
            row_sum = small.tile([P, 2], F32)
            for h in range(2):
                nc.scalar.activation(
                    out=expd[:, h, :],
                    in_=scaled[:, h, :],
                    func=ACT.Exp,
                    bias=shift[:, h : h + 1],
                    scale=-1.0,
                    accum_out=row_sum[:, h : h + 1],
                )
            exps[step] = (expd, row_sum)

        def reciprocals(step):
            expd, row_sum = exps[step]
            inv_sum = small.tile([P, 2], F32)
            nc.vector.reciprocal(out=inv_sum[:], in_=row_sum[:])
            exps[step] = (expd, inv_sum)

        def normalise(step, h):
            expd, inv_sum = exps[step]
            if h == 0:
                softmaxes[step] = work.tile([P, 2, S], F32, bufs=5, name="normed")
            engine = nc.vector if step >= STEPS - 2 else nc.gpsimd
            engine.tensor_scalar(
                out=softmaxes[step][:, h, :], in0=expd[:, h, :], scalar1=inv_sum[:, h : h + 1],
                scalar2=neg_lam[:, 0:1] if h == 1 else 1.0, op0=ALU.mult, op1=ALU.mult,
            )

        def difference_transposed(step, h):
            normed = softmaxes[step]
            if h == 0:
                attn_T[step] = psum.tile([P, TILES, P], F32, name="aT_ps", bufs=2)
            aT_ps = attn_T[step]
            for t in range(TILES):
                nc.tensor.matmul(
                    out=aT_ps[:, t, :],
                    lhsT=normed[:, h, t * P : (t + 1) * P],
                    rhs=ident_f32[:],
                    start=(h == 0 and t == 0),
                    stop=(h == 1 and t == TILES - 1),
                    is_transpose=True,
                )

        def copy_attn(step, copy):
            b, j = divmod(step, TILES)
            if j == 0:
                a_mx[b] = batch.tile([P, TILES * P * 4], BF16, name="a_grouped", align_bytes=64)
            a_grouped = a_mx[b][:].rearrange("p (j q t) -> p j q t", j=TILES, t=TILES)
            aT_ps = attn_T.pop(step)
            copy(out=a_grouped[:, j, :, :], in_=aT_ps[:].rearrange("p t q -> p q t"))

        SV = (nc.scalar.copy, nc.vector.tensor_copy)
        plan = {}

        def at(rnd, slot, stage, *args):
            plan.setdefault((rnd, slot), []).append((stage, args))

        at(-9, "warm", warm_up, 16)
        for b in range(B):
            r = TILES * b
            last = b == B - 1
            at(r - 8, "load", load, b)
            at(r + (-5), "transpose", transpose_head, b, "k")
            at(r + (-5), "copy T", copy_head, b, "k", SV[0])
            at(r + (-4), "transpose", transpose_head, b, "q")
            at(r + (-3), "copy T", copy_head, b, "q", SV[0])
            at(r + (-3), "transpose", transpose_x, b, 0)
            at(r + (-2), "copy T", copy_x, b, 0, SV[0])
            at(r + (-2), "transpose", transpose_x, b, 1)
            at(r + (-2), "copy T", copy_x, b, 1, SV[0])
            at(r + (2 if last else 3), "mx v", project_v, b, 0)
            at(r + (2 if last else 3), "copy V", copy_v, b, 0, SV[0])
            at(r + (2 if last else 3), "mx v", project_v, b, 1)
            at(r + (2 if last else 3), "copy V", copy_v, b, 1, SV[0])
            if not last:
                at(r + (8), "mx o", output, b, 2 * 0, 2)
                at(r + (8), "copy O", copy_output, b, 2 * 0, 2, SV[0])
            if not last:
                at(r + (8), "mx o", output, b, 2 * 1, 2)
                at(r + (9), "copy O", copy_output, b, 2 * 1, 2, SV[0])
            at(r + (-1), "quantise x", quantise_x, b)
            at(r + (5 if last else 6), "quantise v", quantise_v, b)
            if not last:
                at(r + (7), "quantise a", quantise_attn, b, 0, TILES)
        for s in range(STEPS):
            at(s - 2, "score 0", score_matmul, s, 0)
            at(s - 2, "score 1", score_matmul, s, 1)
            at(s - 1, "negate", negate_scores, s)
            at(s, "exp", exponentials, s)
            at(s + 1, "reciprocal", reciprocals, s)
            for h in range(2):
                at(s + 1, "normalise", normalise, s, h)
                at(s + 2, "attn", difference_transposed, s, h)
            at(s + 3, "copy attn", copy_attn, s, SV[0] if False else SV[1])
        for rnd, first, tiles in ((STEPS + 2, 0, 2), (STEPS + 3, 2, 1), (STEPS + 4, 3, 1)):
            at(rnd, "tail", quantise_attn, B - 1, first, tiles)
            at(rnd, "tail", output, B - 1, first, tiles)
            at(rnd, "tail", copy_output, B - 1, first, tiles, SV[0])
        for i in range(4):
            at(STEPS - 2 + i, "score 0", keep_warm)
            at(STEPS - 2 + i, "score 1", keep_warm)
        ORDER = ("load", "exp", "tail", "reciprocal", "attn", "copy attn", "negate", "mx o", "mx v", "normalise", "transpose", "quantise a", "quantise x", "score 0", "warm", "score 1", "copy V", "copy T", "quantise v", "copy O")
        with tc.manual_schedule():
            for i in range(-9, STEPS + 10):
                for slot in ORDER:
                    for stage, args in plan.get((i, slot), []):
                        stage(*args)
